import numpy as np
import ml_dtypes


def mxq(x, axis, fmt="e4m3"):
    dtype, down = {"e4m3": (ml_dtypes.float8_e4m3fn, 7), "e5m2": (ml_dtypes.float8_e5m2, 14)}[fmt]
    v = np.moveaxis(np.asarray(x, np.float32).astype(ml_dtypes.bfloat16).astype(np.float64), axis, -1)
    blocks = v.reshape(v.shape[:-1] + (-1, 32))
    amax = np.abs(blocks).max(-1, keepdims=True)
    byte = np.maximum(np.where(amax > 0, np.frexp(amax)[1] - 1 + 127, 0) - down, 1)
    scale = np.exp2(byte - 127.0)
    codes = (blocks / scale).astype(np.float32).astype(dtype).astype(np.float64)
    return np.moveaxis((codes * scale).reshape(v.shape), -1, axis)


WIDE = False


def mx_kscale(k):
    if not WIDE:
        return np.ones(k)
    levels = np.array([10, -10, 5, -5, 0])
    if k % 512:
        return np.exp2(np.random.permutation(np.resize(levels, k // 32))).repeat(32)
    a = np.empty((k // 512, 16))
    for p in range(k // 512):
        a[p, :8] = np.random.permutation(np.resize(levels, 8))
        for g in range(8):
            far = levels[np.abs(levels - a[p, g]) >= 10]
            a[p, g + 8] = far[np.random.randint(len(far))]
    return np.exp2(a.ravel()).repeat(32)


BF16 = ml_dtypes.bfloat16


def bf(x):
    return np.asarray(x, np.float32).astype(BF16)


def f64(x):
    return np.asarray(x).astype(np.float64)


B, V, H = 512, 128, 1024
G = 4 * H
EPS = 1e-5


def sigmoid(v):
    return 1.0 / (1.0 + np.exp(-v))


def layer_norm(v, w, b):
    mu = v.mean(-1, keepdims=True)
    var = ((v - mu) ** 2).mean(-1, keepdims=True)
    return (v - mu) / np.sqrt(var + EPS) * w + b


def draw0():
    s = mx_kscale(H)
    return {"x": bf(np.random.standard_normal((B, V))),
            "h0": bf(np.random.standard_normal((B, H)) * s),
            "c0": bf(np.random.standard_normal((B, H))),
            "w_ih1": bf(np.random.standard_normal((G, V)) / np.sqrt(V)),
            "w_hh1": bf(np.random.standard_normal((G, H)) / np.sqrt(H) / s),
            "lni_w1": bf(1.0 + 0.1 * np.random.standard_normal(G)),
            "lni_b1": bf(0.1 * np.random.standard_normal(G)),
            "lnh_w1": bf(1.0 + 0.1 * np.random.standard_normal(G)),
            "lnh_b1": bf(0.1 * np.random.standard_normal(G)),
            "lnc_w1": bf(1.0 + 0.1 * np.random.standard_normal(H)),
            "lnc_b1": bf(0.1 * np.random.standard_normal(H))}


def core(x, h0, c0, w_ih1, w_hh1, lni_w1, lni_b1, lnh_w1, lnh_b1, lnc_w1, lnc_b1):
    a = f64(x) @ f64(w_ih1).T
    r = mxq(f64(h0), 1, "e4m3") @ mxq(f64(w_hh1), 1, "e4m3").T
    gates = layer_norm(a, f64(lni_w1), f64(lni_b1)) + layer_norm(r, f64(lnh_w1), f64(lnh_b1))
    i, f, g, o = np.split(gates, 4, axis=1)
    cy = layer_norm(sigmoid(f) * f64(c0) + sigmoid(i) * np.tanh(g), f64(lnc_w1), f64(lnc_b1))
    hy = sigmoid(o) * np.tanh(cy)
    return hy, cy


def e4m3fn_bytes(y):
    return np.clip(np.asarray(y, np.float64), -448.0, 448.0).astype(np.float32).astype(ml_dtypes.float8_e4m3fn).view(np.uint8)


def e4m3fn_values(b):
    return np.asarray(b, np.uint8).view(ml_dtypes.float8_e4m3fn).astype(np.float64)


def setup_inputs():
    d = draw0()
    x0 = np.asarray(d['w_hh1']).astype(np.float64)
    s = (np.max(np.abs(x0), axis=(0,), keepdims=True) / 448.0).astype(np.float32)
    out = {}
    for k, v in d.items():
        if k == 'w_hh1':
            out['w_hh1_bytes'] = e4m3fn_bytes(x0 / s.astype(np.float64))
            out['w_hh1_scale'] = s
        else:
            out[k] = v
    return out


def reference(x, h0, c0, w_ih1, w_hh1_bytes, w_hh1_scale, lni_w1, lni_b1, lnh_w1, lnh_b1, lnc_w1, lnc_b1):
    return core(x, h0, c0, w_ih1, e4m3fn_values(w_hh1_bytes) * w_hh1_scale.astype(np.float64), lni_w1, lni_b1, lnh_w1, lnh_b1, lnc_w1, lnc_b1)

@@ -1,0 +1,406 @@
+from contextlib import ExitStack
+
+import concourse.mybir as mybir
+from concourse.masks import make_identity
+
+B, V, H = 512, 128, 1024
+G = 4 * H
+EPS = 1e-5
+FLOPS = 2 * B * G * (H + V)
+
+F32 = mybir.dt.float32
+BF16 = mybir.dt.bfloat16
+U8 = mybir.dt.uint8
+U32 = mybir.dt.uint32
+FP8 = mybir.dt.float8_e4m3fn
+FP8X4 = mybir.dt.float8_e4m3fn_x4
+ALU = mybir.AluOpType
+ACT = mybir.ActivationFunctionType
+AX = mybir.AxisListType
+
+P = 128
+NT = B // P
+CH = 512
+NCH = G // CH
+JT = CH // P
+NJ = G // P
+
+
+def tile_multilstm_pa_kernel(
+    tc, x, h0, c0, w_ih1, w_hh1_bytes, w_hh1_scale,
+    lni_w1, lni_b1, lnh_w1, lnh_b1, lnc_w1, lnc_b1, out_0, out_1,
+):
+    nc = tc.nc
+    with ExitStack() as ctx:
+        main = ctx.enter_context(tc.tile_pool(name="main", bufs=1))
+        psum = ctx.enter_context(tc.psum_pool(name="psum", bufs=1))
+
+        scale_bc = main.tile([P, H], F32, name="scale_bc")
+        wh_bc = main.tile([P, G], BF16, name="wh_bc")
+        bt = main.tile([P, NJ, P], F32, name="bt")
+        lncw_bc = main.tile([P, H], BF16, name="lncw_bc")
+        lncb_bc = main.tile([P, H], BF16, name="lncb_bc")
+        wpT = main.tile([P, G], F32, name="wpT")
+        xT = main.tile([P, B], F32, name="xT")
+        xs = main.tile([P, NT, V], F32, name="xs")
+        xsT = main.tile([P, B], F32, name="xsT")
+        x_nat = main.tile([P, NT, V], BF16, name="x_nat")
+        c_sb = main.tile([P, V], F32, name="c_sb")
+        hcod = main.tile([P, 2, B], U32, name="hcod", align_bytes=64)
+        hscl = main.tile([P, 2, B], U8, name="hscl", align_bytes=64)
+        ring = [main.tile([P, G], F32, name="ring%d" % t) for t in range(NT + 1)]
+        r_sb = ring[0:NT]
+        g_sb = [ring[NT]] + ring[0:NT - 1]
+        rsum = main.tile([P, NT, NCH], F32, name="rsum")
+        rtot = main.tile([P, NT], F32, name="rtot")
+        negmu = main.tile([P, NT], F32, name="negmu")
+        rvs = main.tile([P, NT], F32, name="rvs")
+        rve = main.tile([P, NT], F32, name="rve")
+        a_r = main.tile([P, NT], F32, name="a_r")
+        va = main.tile([P, NT], F32, name="va")
+        vae = main.tile([P, NT], F32, name="vae")
+        a_a = main.tile([P, NT], F32, name="a_a")
+        csum = main.tile([P, NT], F32, name="csum")
+        negmuc = main.tile([P, NT], F32, name="negmuc")
+        cvs = main.tile([P, NT], F32, name="cvs")
+        cve = main.tile([P, NT], F32, name="cve")
+        a_c = main.tile([P, NT], F32, name="a_c")
+        wsum = main.tile([P, NCH], F32, name="wsum")
+        wtot = main.tile([P, 1], F32, name="wtot")
+        negwbar = main.tile([P, 1], F32, name="negwbar")
+        bcols = main.tile([P, 2 * NJ], F32, name="bcols")
+        bsum_col = main.tile([P, NJ], F32, name="bsum_col")
+
+        wb_tiles = {}
+
+        def load_w(c, pieces):
+            wb = main.tile([P, JT, H], U8, name="wb", tag="wb", bufs=3)
+            src = w_hh1_bytes[c * CH:(c + 1) * CH, :].rearrange("(j p) k -> p j k", p=P)
+            step_j = JT // pieces
+            for i in range(pieces):
+                nc.sync.dma_start(
+                    out=wb[:, i * step_j:(i + 1) * step_j, :], in_=src[:, i * step_j:(i + 1) * step_j, :]
+                )
+            wb_tiles[c] = wb
+
+        nc.sync.dma_start(
+            out=scale_bc[:], in_=w_hh1_scale.rearrange("o k -> (o k)").partition_broadcast(P)
+        )
+        load_w(0, JT)
+        load_w(1, 1)
+
+        neg_half = main.tile([P, NT], F32, name="neg_half")
+        nc.vector.memset(neg_half[:], -0.5)
+        ident_f = main.tile([P, P], F32, name="ident_f")
+        make_identity(nc, ident_f[:])
+        ident_b = main.tile([P, P], BF16, name="ident_b")
+        make_identity(nc, ident_b[:])
+
+        def flip(words, grouped_words, col0):
+            tp = psum.tile([P, 4, P], F32, name="tp", tag="tp", bufs=3)
+            for g2 in range(2):
+                for u in range(2):
+                    nc.tensor.transpose(
+                        tp[:, 2 * g2 + u, :],
+                        words[:, 256 * g2 + u:256 * (g2 + 1):2],
+                        ident_f[:],
+                    )
+            nc.scalar.copy(
+                out=grouped_words[:, :, col0:col0 + P, :],
+                in_=tp[:].rearrange("p (g u) r -> p g r u", u=2),
+            )
+
+        grouped_tiles = {}
+
+        def widen_flip(c):
+            wb = wb_tiles[c]
+            grouped = main.tile([P, 2, 4 * CH], BF16, name="grouped", tag="grouped", bufs=2, align_bytes=64)
+            gw = grouped[:].bitcast(F32).rearrange("p g (c u) -> p g c u", u=2)
+            for j in range(JT):
+                wbf = main.tile([P, H], BF16, name="wbf", tag="wbf", bufs=4)
+                nc.vector.tensor_tensor(
+                    out=wbf[:], in0=wb[:, j, :].bitcast(FP8), in1=scale_bc[:], op=ALU.mult
+                )
+                flip(wbf[:].bitcast(F32), gw, j * P)
+            grouped_tiles[c] = grouped
+
+        def quant_mult(c):
+            grouped = grouped_tiles[c]
+            wcod = main.tile([P, 2, CH], U32, name="wcod", tag="wcod", bufs=2, align_bytes=64)
+            wscl = main.tile([P, 2, CH], U8, name="wscl", tag="wscl", bufs=2, align_bytes=64)
+            nc.vector.quantize_mx(
+                out=wcod[:].rearrange("p g c -> p (g c)").bitcast(FP8X4),
+                scales=wscl[:].rearrange("p g c -> p (g c)"),
+                in_=grouped[:].rearrange("p g c -> p (g c)"),
+            )
+            for t in range(NT):
+                mm = psum.tile([P, CH], F32, name="mm", tag="mm", bufs=3)
+                for g2 in range(2):
+                    nc.tensor.matmul_mx(
+                        out=mm[:],
+                        lhsT=hcod[:, g2, t * P:(t + 1) * P].bitcast(FP8X4),
+                        lhsT_scale=hscl[:, g2, t * P:(t + 1) * P],
+                        rhs=wcod[:, g2, :].bitcast(FP8X4),
+                        rhs_scale=wscl[:, g2, :],
+                        start=(g2 == 0),
+                        stop=(g2 == 1),
+                    )
+                nc.scalar.activation(
+                    out=r_sb[t][:, c * CH:(c + 1) * CH], in_=mm[:], func=ACT.Copy,
+                    accum_out=rsum[:, t, c:c + 1],
+                )
+
+        def step(c):
+            if c + 2 < NCH:
+                load_w(c + 2, 1)
+            if c < NCH:
+                widen_flip(c)
+            if c >= 1:
+                quant_mult(c - 1)
+
+        with tc.tile_pool(name="tmpa", bufs=1) as tmpa:
+            h0raw = tmpa.tile([P, NT, H], BF16, name="h0raw")
+            nc.scalar.dma_start(out=h0raw[:], in_=h0.rearrange("(t p) k -> p t k", p=P))
+            warm = tmpa.tile([P, 1], F32, name="warm")
+            nc.scalar.activation(out=warm[:], in_=neg_half[:, 0:1], func=ACT.Sigmoid)
+            colsrc = tmpa.tile([P, P], BF16, name="colsrc")
+            nc.gpsimd.memset(colsrc[:], 0.0)
+            nc.gpsimd.dma_start(out=colsrc[0:NJ, :], in_=lni_b1.rearrange("(j p) -> j p", p=P))
+            nc.gpsimd.dma_start(out=colsrc[NJ:2 * NJ, :], in_=lnh_b1.rearrange("(j p) -> j p", p=P))
+            nc.gpsimd.dma_start(out=x_nat[:], in_=x.rearrange("(t p) v -> p t v", p=P))
+
+            grouped_h = tmpa.tile([P, 2, 4 * B], BF16, name="grouped_h", align_bytes=64)
+            ghw = grouped_h[:].bitcast(F32).rearrange("p g (c u) -> p g c u", u=2)
+            for t in range(NT):
+                flip(h0raw[:, t, :].bitcast(F32), ghw, t * P)
+            nc.vector.quantize_mx(
+                out=hcod[:].rearrange("p g c -> p (g c)").bitcast(FP8X4),
+                scales=hscl[:].rearrange("p g c -> p (g c)"),
+                in_=grouped_h[:].rearrange("p g c -> p (g c)"),
+            )
+            step(0)
+            cps = psum.tile([P, P], BF16, name="cps", tag="misc", bufs=2)
+            nc.tensor.transpose(cps[:], colsrc[:], ident_b[:])
+            nc.scalar.copy(out=bcols[:], in_=cps[:, 0:2 * NJ])
+            nc.vector.tensor_tensor(
+                out=bsum_col[:], in0=bcols[:, 0:NJ], in1=bcols[:, NJ:2 * NJ], op=ALU.add
+            )
+            nc.scalar.activation(
+                out=bt[:], in_=bsum_col[:].unsqueeze(2).to_broadcast([P, NJ, P]), func=ACT.Copy
+            )
+
+        with tc.tile_pool(name="tmpb", bufs=1) as tmpb:
+            w_nat = tmpb.tile([P, NJ, V], BF16, name="w_nat")
+            nc.gpsimd.dma_start(out=w_nat[:], in_=w_ih1.rearrange("(j p) v -> p j v", p=P))
+            wi_bc = tmpb.tile([P, G], BF16, name="wi_bc")
+            nc.gpsimd.dma_start(out=wi_bc[:], in_=lni_w1.partition_broadcast(P))
+            nc.gpsimd.dma_start(out=wh_bc[:], in_=lnh_w1.partition_broadcast(P))
+            nc.gpsimd.dma_start(out=lncw_bc[:], in_=lnc_w1.partition_broadcast(P))
+            nc.gpsimd.dma_start(out=lncb_bc[:], in_=lnc_b1.partition_broadcast(P))
+            w_t = tmpb.tile([P, G], BF16, name="w_t")
+            wc = tmpb.tile([P, NJ, V], F32, name="wc")
+
+            step(1)
+
+            xps = psum.tile([P, NT, P], BF16, name="xps", tag="misc", bufs=2)
+            for t in range(NT):
+                nc.tensor.transpose(xps[:, t, :], x_nat[:, t, :], ident_b[:])
+            nc.scalar.copy(out=xT[:], in_=xps[:].rearrange("p t b -> p (t b)"))
+            for i in range(NCH):
+                wps = psum.tile([P, JT, P], BF16, name="wps", tag="misc", bufs=2)
+                for q in range(JT):
+                    nc.tensor.transpose(wps[:, q, :], w_nat[:, JT * i + q, :], ident_b[:])
+                nc.scalar.activation(
+                    out=w_t[:, i * CH:(i + 1) * CH], in_=wps[:].rearrange("p q g -> p (q g)"),
+                    func=ACT.Copy, accum_out=wsum[:, i:i + 1],
+                )
+
+            step(2)
+
+            nc.vector.tensor_reduce(out=wtot[:], in_=wsum[:], axis=AX.X, op=ALU.add)
+            nc.vector.tensor_scalar(
+                out=negwbar[:], in0=wtot[:], scalar1=-1.0 / G, scalar2=None, op0=ALU.mult
+            )
+            nb = psum.tile([P, V], F32, name="nb", tag="misc", bufs=2)
+            nc.tensor.matmul(
+                nb[:], lhsT=negwbar[:, 0:1].to_broadcast([P, P]), rhs=ident_f[:], start=True, stop=True
+            )
+            nc.vector.tensor_tensor(
+                out=wc[:], in0=w_nat[:], in1=nb[:].unsqueeze(1).to_broadcast([P, NJ, V]), op=ALU.add
+            )
+            gm = psum.tile([P, V], F32, name="gm", tag="misc", bufs=2)
+            for j in range(NJ):
+                nc.tensor.matmul(
+                    gm[:], lhsT=wc[:, j, :], rhs=wc[:, j, :], start=(j == 0), stop=(j == NJ - 1)
+                )
+            nc.scalar.activation(out=c_sb[:], in_=gm[:], func=ACT.Copy, scale=1.0 / G)
+
+            step(3)
+
+            nc.vector.scalar_tensor_tensor(
+                out=wpT[:], in0=w_t[:], scalar=negwbar[:, 0:1], in1=wi_bc[:],
+                op0=ALU.add, op1=ALU.mult,
+            )
+            for t in range(NT):
+                yp = psum.tile([P, V], F32, name="yp", tag="misc", bufs=2)
+                nc.tensor.matmul(yp[:], lhsT=xT[:, t * P:(t + 1) * P], rhs=c_sb[:], start=True, stop=True)
+                ysc = tmpb.tile([P, V], F32, name="ysc", tag="ysc", bufs=2)
+                nc.vector.scalar_tensor_tensor(
+                    out=ysc[:], in0=yp[:], scalar=1.0, in1=x_nat[:, t, :],
+                    op0=ALU.mult, op1=ALU.mult, accum_out=va[:, t:t + 1],
+                )
+            nc.vector.tensor_scalar(out=vae[:], in0=va[:], scalar1=EPS, scalar2=None, op0=ALU.add)
+            nc.gpsimd.tensor_tensor(out=a_a[:], in0=vae[:], in1=neg_half[:], op=ALU.pow)
+
+            step(4)
+
+            for t in range(NT):
+                nc.scalar.activation(
+                    out=xs[:, t, :], in_=x_nat[:, t, :], func=ACT.Copy, scale=a_a[:, t:t + 1]
+                )
+            xsps = psum.tile([P, NT, P], F32, name="xsps", tag="misc", bufs=2)
+            for t in range(NT):
+                nc.tensor.transpose(xsps[:, t, :], xs[:, t, :], ident_f[:])
+            nc.scalar.copy(out=xsT[:], in_=xsps[:].rearrange("p t b -> p (t b)"))
+
+        with tc.tile_pool(name="late", bufs=1) as late:
+            step(5)
+            c0_tiles = []
+            for t in range(NT):
+                c0t = late.tile([P, H], BF16, name="c0t%d" % t)
+                nc.sync.dma_start(out=c0t[:], in_=c0[t * P:(t + 1) * P, :])
+                c0_tiles.append(c0t)
+            for c in range(6, NCH + 1):
+                step(c)
+
+            def stats_r(t):
+                nc.vector.tensor_reduce(out=rtot[:, t:t + 1], in_=rsum[:, t, :], axis=AX.X, op=ALU.add)
+                nc.vector.tensor_scalar(
+                    out=negmu[:, t:t + 1], in0=rtot[:, t:t + 1], scalar1=-1.0 / G, scalar2=None,
+                    op0=ALU.mult,
+                )
+
+            def var_r(t):
+                junk = late.tile([P, G], BF16, name="junk", tag="junk", bufs=1)
+                nc.scalar.activation(
+                    out=junk[:], in_=r_sb[t][:], func=ACT.Square, bias=negmu[:, t:t + 1], scale=1.0,
+                    accum_out=rvs[:, t:t + 1],
+                )
+
+            def rstd_r(t):
+                nc.vector.tensor_scalar(
+                    out=rve[:, t:t + 1], in0=rvs[:, t:t + 1], scalar1=1.0 / G, scalar2=EPS,
+                    op0=ALU.mult, op1=ALU.add,
+                )
+                nc.gpsimd.tensor_tensor(
+                    out=a_r[:, t:t + 1], in0=rve[:, t:t + 1], in1=neg_half[:, 0:1], op=ALU.pow
+                )
+
+            def gain_r(t):
+                nc.vector.scalar_tensor_tensor(
+                    out=g_sb[t][:], in0=r_sb[t][:], scalar=negmu[:, t:t + 1], in1=wh_bc[:],
+                    op0=ALU.add, op1=ALU.mult,
+                )
+
+            def gates(t):
+                gt = g_sb[t]
+                for c in range(NCH):
+                    dps = psum.tile([P, CH], F32, name="dps", tag=("mm", "tp")[c % 2], bufs=3)
+                    nc.tensor.matmul(
+                        dps[:], lhsT=xsT[:, t * P:(t + 1) * P], rhs=wpT[:, c * CH:(c + 1) * CH],
+                        start=True, stop=False,
+                    )
+                    for q in range(JT):
+                        nc.tensor.matmul(
+                            dps[:, q * P:(q + 1) * P], lhsT=bt[:, JT * c + q, :], rhs=ident_f[:],
+                            is_transpose=True, start=False, stop=(q == JT - 1),
+                        )
+                    nc.vector.scalar_tensor_tensor(
+                        out=gt[:, c * CH:(c + 1) * CH], in0=gt[:, c * CH:(c + 1) * CH],
+                        scalar=a_r[:, t:t + 1], in1=dps[:], op0=ALU.mult, op1=ALU.add,
+                    )
+                    if c == 3:
+                        nc.scalar.activation(out=gt[:, 0:2 * H], in_=gt[:, 0:2 * H], func=ACT.Sigmoid)
+                    if c == 5:
+                        nc.scalar.activation(out=gt[:, 2 * H:3 * H], in_=gt[:, 2 * H:3 * H], func=ACT.Tanh)
+                    if c == 7:
+                        nc.scalar.activation(out=gt[:, 3 * H:4 * H], in_=gt[:, 3 * H:4 * H], func=ACT.Sigmoid)
+
+            def cell(t):
+                gt = g_sb[t]
+                s_i = gt[:, 0:H]
+                s_f = gt[:, H:2 * H]
+                t_g = gt[:, 2 * H:3 * H]
+                nc.vector.tensor_tensor(out=s_f, in0=s_f, in1=c0_tiles[t][:], op=ALU.mult)
+                nc.vector.tensor_tensor(out=s_i, in0=s_i, in1=t_g, op=ALU.mult)
+                nc.vector.scalar_tensor_tensor(
+                    out=t_g, in0=s_i, scalar=1.0, in1=s_f, op0=ALU.mult, op1=ALU.add,
+                    accum_out=csum[:, t:t + 1],
+                )
+                nc.vector.tensor_scalar(
+                    out=negmuc[:, t:t + 1], in0=csum[:, t:t + 1], scalar1=-1.0 / H, scalar2=None,
+                    op0=ALU.mult,
+                )
+                junkc = late.tile([P, H], BF16, name="junkc", tag="junkc", bufs=1)
+                nc.scalar.activation(
+                    out=junkc[:], in_=t_g, func=ACT.Square, bias=negmuc[:, t:t + 1], scale=1.0,
+                    accum_out=cvs[:, t:t + 1],
+                )
+                nc.vector.tensor_scalar(
+                    out=cve[:, t:t + 1], in0=cvs[:, t:t + 1], scalar1=1.0 / H, scalar2=EPS,
+                    op0=ALU.mult, op1=ALU.add,
+                )
+                nc.gpsimd.tensor_tensor(
+                    out=a_c[:, t:t + 1], in0=cve[:, t:t + 1], in1=neg_half[:, 0:1], op=ALU.pow
+                )
+
+            def norm_c(t):
+                gt = g_sb[t]
+                s_i = gt[:, 0:H]
+                s_f = gt[:, H:2 * H]
+                t_g = gt[:, 2 * H:3 * H]
+                nc.vector.scalar_tensor_tensor(
+                    out=s_i, in0=t_g, scalar=negmuc[:, t:t + 1], in1=lncw_bc[:],
+                    op0=ALU.add, op1=ALU.mult,
+                )
+                nc.vector.scalar_tensor_tensor(
+                    out=s_f, in0=s_i, scalar=a_c[:, t:t + 1], in1=lncb_bc[:],
+                    op0=ALU.mult, op1=ALU.add,
+                )
+                nc.sync.dma_start(out=out_1[t * P:(t + 1) * P, :], in_=s_f)
+                nc.scalar.activation(out=s_i, in_=s_f, func=ACT.Tanh)
+
+            def hidden(t):
+                gt = g_sb[t]
+                nc.vector.tensor_tensor(
+                    out=gt[:, 2 * H:3 * H], in0=gt[:, 3 * H:4 * H], in1=gt[:, 0:H], op=ALU.mult
+                )
+                nc.sync.dma_start(out=out_0[t * P:(t + 1) * P, :], in_=gt[:, 2 * H:3 * H])
+
+            for t in range(NT):
+                stats_r(t)
+                var_r(t)
+            gain_r(0)
+            rstd_r(0)
+            gain_r(1)
+            rstd_r(1)
+            gates(0)
+            gain_r(2)
+            rstd_r(2)
+            gates(1)
+            cell(0)
+            gain_r(3)
+            rstd_r(3)
+            gates(2)
+            cell(1)
+            norm_c(0)
+            gates(3)
+            cell(2)
+            norm_c(1)
+            hidden(0)
+            cell(3)
+            norm_c(2)
+            hidden(1)
+            norm_c(3)
+            hidden(2)
+            hidden(3)

@@ -24,6 +24,7 @@ CH = 512
 NCH = G // CH
 JT = CH // P
 NJ = G // P
+VPAD = 144
 
 
 def tile_multilstm_pa_kernel(
@@ -37,7 +38,6 @@ def tile_multilstm_pa_kernel(
 
         scale_bc = main.tile([P, H], F32, name="scale_bc")
         wh_bc = main.tile([P, G], BF16, name="wh_bc")
-        bt = main.tile([P, NJ, P], F32, name="bt")
         lncw_bc = main.tile([P, H], BF16, name="lncw_bc")
         lncb_bc = main.tile([P, H], BF16, name="lncb_bc")
         wpT = main.tile([P, G], F32, name="wpT")
@@ -65,8 +65,6 @@ def tile_multilstm_pa_kernel(
         cvs = main.tile([P, NT], F32, name="cvs")
         cve = main.tile([P, NT], F32, name="cve")
         a_c = main.tile([P, NT], F32, name="a_c")
-        wsum = main.tile([P, NCH], F32, name="wsum")
-        wtot = main.tile([P, 1], F32, name="wtot")
         negwbar = main.tile([P, 1], F32, name="negwbar")
         bcols = main.tile([P, 2 * NJ], F32, name="bcols")
         bsum_col = main.tile([P, NJ], F32, name="bsum_col")
@@ -185,20 +183,18 @@ def tile_multilstm_pa_kernel(
             nc.vector.tensor_tensor(
                 out=bsum_col[:], in0=bcols[:, 0:NJ], in1=bcols[:, NJ:2 * NJ], op=ALU.add
             )
-            nc.scalar.activation(
-                out=bt[:], in_=bsum_col[:].unsqueeze(2).to_broadcast([P, NJ, P]), func=ACT.Copy
-            )
 
         with tc.tile_pool(name="tmpb", bufs=1) as tmpb:
-            w_nat = tmpb.tile([P, NJ, V], BF16, name="w_nat")
-            nc.gpsimd.dma_start(out=w_nat[:], in_=w_ih1.rearrange("(j p) v -> p j v", p=P))
+            w_nat = tmpb.tile([P, NJ, VPAD], BF16, name="w_nat")
+            nc.vector.memset(w_nat[:, :, V:V + 2], 1.0)
+            nc.gpsimd.dma_start(out=w_nat[:, :, 0:V], in_=w_ih1.rearrange("(j p) v -> p j v", p=P))
             wi_bc = tmpb.tile([P, G], BF16, name="wi_bc")
             nc.gpsimd.dma_start(out=wi_bc[:], in_=lni_w1.partition_broadcast(P))
             nc.gpsimd.dma_start(out=wh_bc[:], in_=lnh_w1.partition_broadcast(P))
             nc.gpsimd.dma_start(out=lncw_bc[:], in_=lnc_w1.partition_broadcast(P))
             nc.gpsimd.dma_start(out=lncb_bc[:], in_=lnc_b1.partition_broadcast(P))
             w_t = tmpb.tile([P, G], BF16, name="w_t")
-            wc = tmpb.tile([P, NJ, V], F32, name="wc")
+            craw = tmpb.tile([P, V + 2], F32, name="craw")
 
             step(1)
 
@@ -206,34 +202,34 @@ def tile_multilstm_pa_kernel(
             for t in range(NT):
                 nc.tensor.transpose(xps[:, t, :], x_nat[:, t, :], ident_b[:])
             nc.scalar.copy(out=xT[:], in_=xps[:].rearrange("p t b -> p (t b)"))
+            gm = psum.tile([P, V + 2], F32, name="gm", tag="misc", bufs=2)
+            for j in range(NJ):
+                nc.tensor.matmul(
+                    gm[:], lhsT=w_nat[:, j, 0:V], rhs=w_nat[:, j, 0:V + 2],
+                    start=(j == 0), stop=(j == NJ - 1),
+                )
+            nc.scalar.activation(out=craw[:], in_=gm[:], func=ACT.Copy, scale=1.0 / G)
             for i in range(NCH):
                 wps = psum.tile([P, JT, P], BF16, name="wps", tag="misc", bufs=2)
                 for q in range(JT):
-                    nc.tensor.transpose(wps[:, q, :], w_nat[:, JT * i + q, :], ident_b[:])
-                nc.scalar.activation(
-                    out=w_t[:, i * CH:(i + 1) * CH], in_=wps[:].rearrange("p q g -> p (q g)"),
-                    func=ACT.Copy, accum_out=wsum[:, i:i + 1],
+                    nc.tensor.transpose(wps[:, q, :], w_nat[:, JT * i + q, 0:V], ident_b[:])
+                nc.scalar.copy(
+                    out=w_t[:, i * CH:(i + 1) * CH], in_=wps[:].rearrange("p q g -> p (q g)")
                 )
 
             step(2)
 
-            nc.vector.tensor_reduce(out=wtot[:], in_=wsum[:], axis=AX.X, op=ALU.add)
             nc.vector.tensor_scalar(
-                out=negwbar[:], in0=wtot[:], scalar1=-1.0 / G, scalar2=None, op0=ALU.mult
+                out=negwbar[:], in0=craw[:, V:V + 1], scalar1=-1.0, scalar2=None, op0=ALU.mult
             )
             nb = psum.tile([P, V], F32, name="nb", tag="misc", bufs=2)
             nc.tensor.matmul(
                 nb[:], lhsT=negwbar[:, 0:1].to_broadcast([P, P]), rhs=ident_f[:], start=True, stop=True
             )
-            nc.vector.tensor_tensor(
-                out=wc[:], in0=w_nat[:], in1=nb[:].unsqueeze(1).to_broadcast([P, NJ, V]), op=ALU.add
+            nc.vector.scalar_tensor_tensor(
+                out=c_sb[:], in0=nb[:], scalar=craw[:, V:V + 1], in1=craw[:, 0:V],
+                op0=ALU.mult, op1=ALU.add,
             )
-            gm = psum.tile([P, V], F32, name="gm", tag="misc", bufs=2)
-            for j in range(NJ):
-                nc.tensor.matmul(
-                    gm[:], lhsT=wc[:, j, :], rhs=wc[:, j, :], start=(j == 0), stop=(j == NJ - 1)
-                )
-            nc.scalar.activation(out=c_sb[:], in_=gm[:], func=ACT.Copy, scale=1.0 / G)
 
             step(3)
 
@@ -312,7 +308,7 @@ def tile_multilstm_pa_kernel(
                     )
                     for q in range(JT):
                         nc.tensor.matmul(
-                            dps[:, q * P:(q + 1) * P], lhsT=bt[:, JT * c + q, :], rhs=ident_f[:],
+                            dps[:, q * P:(q + 1) * P], lhsT=bsum_col[:, JT * c + q:JT * c + q + 1].to_broadcast([P, P]), rhs=ident_f[:],
                             is_transpose=True, start=False, stop=(q == JT - 1),
                         )
                     nc.vector.scalar_tensor_tensor(

@@ -25,6 +25,8 @@ NCH = G // CH
 JT = CH // P
 NJ = G // P
 VPAD = 144
+BANKS = ("tp", "mm", "gm", "tp", "mm", "misc", "tp", "mm")
+BUFS = {"tp": 3, "mm": 3, "gm": 1, "misc": 1}
 
 
 def tile_multilstm_pa_kernel(
@@ -35,9 +37,14 @@ def tile_multilstm_pa_kernel(
     with ExitStack() as ctx:
         main = ctx.enter_context(tc.tile_pool(name="main", bufs=1))
         psum = ctx.enter_context(tc.psum_pool(name="psum", bufs=1))
+        ctx.enter_context(tc.manual_schedule())
+
+        def bank(shape, dtype, tag):
+            return psum.tile(shape, dtype, name="ps_" + tag, tag=tag, bufs=BUFS[tag])
 
         scale_bc = main.tile([P, H], F32, name="scale_bc")
         wh_bc = main.tile([P, G], BF16, name="wh_bc")
+        wi_bc = main.tile([P, G], BF16, name="wi_bc")
         lncw_bc = main.tile([P, H], BF16, name="lncw_bc")
         lncb_bc = main.tile([P, H], BF16, name="lncb_bc")
         wpT = main.tile([P, G], F32, name="wpT")
@@ -45,7 +52,10 @@ def tile_multilstm_pa_kernel(
         xs = main.tile([P, NT, V], F32, name="xs")
         xsT = main.tile([P, B], F32, name="xsT")
         x_nat = main.tile([P, NT, V], BF16, name="x_nat")
+        ysc = main.tile([P, NT, V], F32, name="ysc")
+        craw = main.tile([P, V + 2], F32, name="craw")
         c_sb = main.tile([P, V], F32, name="c_sb")
+        colsrc = main.tile([P, P], BF16, name="colsrc")
         hcod = main.tile([P, 2, B], U32, name="hcod", align_bytes=64)
         hscl = main.tile([P, 2, B], U8, name="hscl", align_bytes=64)
         ring = [main.tile([P, G], F32, name="ring%d" % t) for t in range(NT + 1)]
@@ -68,11 +78,18 @@ def tile_multilstm_pa_kernel(
         negwbar = main.tile([P, 1], F32, name="negwbar")
         bcols = main.tile([P, 2 * NJ], F32, name="bcols")
         bsum_col = main.tile([P, NJ], F32, name="bsum_col")
+        neg_half = main.tile([P, NT], F32, name="neg_half")
+        warm = main.tile([P, 1], F32, name="warm")
+        ident_f = main.tile([P, P], F32, name="ident_f")
+        ident_b = main.tile([P, P], BF16, name="ident_b")
+        h0raw = main.tile([P, NT, H], BF16, name="h0raw", tag="share_a", bufs=1)
+        grouped_h = main.tile([P, 2, 4 * B], BF16, name="grouped_h", tag="share_b", bufs=1, align_bytes=64)
+        w_nat = main.tile([P, NJ, VPAD], BF16, name="w_nat", tag="share_c", bufs=1)
 
         wb_tiles = {}
 
         def load_w(c, pieces):
-            wb = main.tile([P, JT, H], U8, name="wb", tag="wb", bufs=3)
+            wb = main.tile([P, JT, H], U8, name="wb", tag="wb", bufs=4)
             src = w_hh1_bytes[c * CH:(c + 1) * CH, :].rearrange("(j p) k -> p j k", p=P)
             step_j = JT // pieces
             for i in range(pieces):
@@ -86,317 +103,397 @@ def tile_multilstm_pa_kernel(
         )
         load_w(0, JT)
         load_w(1, 1)
-
-        neg_half = main.tile([P, NT], F32, name="neg_half")
+        nc.sync.dma_start(out=h0raw[:], in_=h0.rearrange("(t p) k -> p t k", p=P))
         nc.vector.memset(neg_half[:], -0.5)
-        ident_f = main.tile([P, P], F32, name="ident_f")
+        nc.vector.memset(w_nat[:, :, V:V + 2], 1.0)
         make_identity(nc, ident_f[:])
-        ident_b = main.tile([P, P], BF16, name="ident_b")
         make_identity(nc, ident_b[:])
+        nc.gpsimd.memset(colsrc[:], 0.0)
+        nc.scalar.activation(out=warm[:], in_=neg_half[:, 0:1], func=ACT.Sigmoid)
+        nc.sync.dma_start(out=x_nat[:], in_=x.rearrange("(t p) v -> p t v", p=P))
+        nc.sync.dma_start(out=colsrc[0:NJ, :], in_=lni_b1.rearrange("(j p) -> j p", p=P))
+        nc.sync.dma_start(out=colsrc[NJ:2 * NJ, :], in_=lnh_b1.rearrange("(j p) -> j p", p=P))
+        load_w(2, 1)
+        nc.sync.dma_start(out=w_nat[:, :, 0:V], in_=w_ih1.rearrange("(j p) v -> p j v", p=P))
+        load_w(3, 1)
+        nc.sync.dma_start(out=wi_bc[:], in_=lni_w1.partition_broadcast(P))
 
-        def flip(words, grouped_words, col0):
-            tp = psum.tile([P, 4, P], F32, name="tp", tag="tp", bufs=3)
+        wbf_tiles = {}
+        tp_tiles = {}
+        grouped_tiles = {}
+        cod_tiles = {}
+        mm_tiles = {}
+
+        def widen(k):
+            wbf = main.tile([P, H], BF16, name="wbf", tag="wbf", bufs=6)
+            nc.vector.tensor_tensor(
+                out=wbf[:], in0=wb_tiles[k // JT][:, k % JT, :].bitcast(FP8), in1=scale_bc[:], op=ALU.mult
+            )
+            wbf_tiles[k] = wbf
+
+        def turn(key, words):
+            tp = bank([P, 4, P], F32, "tp")
             for g2 in range(2):
                 for u in range(2):
                     nc.tensor.transpose(
-                        tp[:, 2 * g2 + u, :],
-                        words[:, 256 * g2 + u:256 * (g2 + 1):2],
-                        ident_f[:],
+                        tp[:, 2 * g2 + u, :], words[:, 256 * g2 + u:256 * (g2 + 1):2], ident_f[:]
                     )
+            tp_tiles[key] = tp
+
+        def copy_out(key, grouped, col0):
+            gw = grouped[:].bitcast(F32).rearrange("p g (c u) -> p g c u", u=2)
             nc.scalar.copy(
-                out=grouped_words[:, :, col0:col0 + P, :],
-                in_=tp[:].rearrange("p (g u) r -> p g r u", u=2),
+                out=gw[:, :, col0:col0 + P, :],
+                in_=tp_tiles[key][:].rearrange("p (g u) r -> p g r u", u=2),
             )
 
-        grouped_tiles = {}
+        def turn_w(k):
+            turn(k, wbf_tiles[k][:].bitcast(F32))
 
-        def widen_flip(c):
-            wb = wb_tiles[c]
-            grouped = main.tile([P, 2, 4 * CH], BF16, name="grouped", tag="grouped", bufs=2, align_bytes=64)
-            gw = grouped[:].bitcast(F32).rearrange("p g (c u) -> p g c u", u=2)
-            for j in range(JT):
-                wbf = main.tile([P, H], BF16, name="wbf", tag="wbf", bufs=4)
-                nc.vector.tensor_tensor(
-                    out=wbf[:], in0=wb[:, j, :].bitcast(FP8), in1=scale_bc[:], op=ALU.mult
+        def copy_w(k):
+            if k % JT == 0:
+                grouped_tiles[k // JT] = main.tile(
+                    [P, 2, 4 * CH], BF16, name="grouped", tag="grouped", bufs=2, align_bytes=64
                 )
-                flip(wbf[:].bitcast(F32), gw, j * P)
-            grouped_tiles[c] = grouped
+            copy_out(k, grouped_tiles[k // JT], (k % JT) * P)
 
-        def quant_mult(c):
-            grouped = grouped_tiles[c]
+        def quant_w(c):
             wcod = main.tile([P, 2, CH], U32, name="wcod", tag="wcod", bufs=2, align_bytes=64)
             wscl = main.tile([P, 2, CH], U8, name="wscl", tag="wscl", bufs=2, align_bytes=64)
             nc.vector.quantize_mx(
                 out=wcod[:].rearrange("p g c -> p (g c)").bitcast(FP8X4),
                 scales=wscl[:].rearrange("p g c -> p (g c)"),
-                in_=grouped[:].rearrange("p g c -> p (g c)"),
+                in_=grouped_tiles[c][:].rearrange("p g c -> p (g c)"),
             )
-            for t in range(NT):
-                mm = psum.tile([P, CH], F32, name="mm", tag="mm", bufs=3)
-                for g2 in range(2):
-                    nc.tensor.matmul_mx(
-                        out=mm[:],
-                        lhsT=hcod[:, g2, t * P:(t + 1) * P].bitcast(FP8X4),
-                        lhsT_scale=hscl[:, g2, t * P:(t + 1) * P],
-                        rhs=wcod[:, g2, :].bitcast(FP8X4),
-                        rhs_scale=wscl[:, g2, :],
-                        start=(g2 == 0),
-                        stop=(g2 == 1),
-                    )
-                nc.scalar.activation(
-                    out=r_sb[t][:, c * CH:(c + 1) * CH], in_=mm[:], func=ACT.Copy,
-                    accum_out=rsum[:, t, c:c + 1],
+            cod_tiles[c] = (wcod, wscl)
+
+        def mult(c, t):
+            wcod, wscl = cod_tiles[c]
+            mm = bank([P, CH], F32, "mm")
+            for g2 in range(2):
+                nc.tensor.matmul_mx(
+                    out=mm[:],
+                    lhsT=hcod[:, g2, t * P:(t + 1) * P].bitcast(FP8X4),
+                    lhsT_scale=hscl[:, g2, t * P:(t + 1) * P],
+                    rhs=wcod[:, g2, :].bitcast(FP8X4),
+                    rhs_scale=wscl[:, g2, :],
+                    start=(g2 == 0),
+                    stop=(g2 == 1),
                 )
+            mm_tiles[(c, t)] = mm
 
-        def step(c):
-            if c + 2 < NCH:
-                load_w(c + 2, 1)
-            if c < NCH:
-                widen_flip(c)
-            if c >= 1:
-                quant_mult(c - 1)
-
-        with tc.tile_pool(name="tmpa", bufs=1) as tmpa:
-            h0raw = tmpa.tile([P, NT, H], BF16, name="h0raw")
-            nc.scalar.dma_start(out=h0raw[:], in_=h0.rearrange("(t p) k -> p t k", p=P))
-            warm = tmpa.tile([P, 1], F32, name="warm")
-            nc.scalar.activation(out=warm[:], in_=neg_half[:, 0:1], func=ACT.Sigmoid)
-            colsrc = tmpa.tile([P, P], BF16, name="colsrc")
-            nc.gpsimd.memset(colsrc[:], 0.0)
-            nc.gpsimd.dma_start(out=colsrc[0:NJ, :], in_=lni_b1.rearrange("(j p) -> j p", p=P))
-            nc.gpsimd.dma_start(out=colsrc[NJ:2 * NJ, :], in_=lnh_b1.rearrange("(j p) -> j p", p=P))
-            nc.gpsimd.dma_start(out=x_nat[:], in_=x.rearrange("(t p) v -> p t v", p=P))
-
-            grouped_h = tmpa.tile([P, 2, 4 * B], BF16, name="grouped_h", align_bytes=64)
-            ghw = grouped_h[:].bitcast(F32).rearrange("p g (c u) -> p g c u", u=2)
-            for t in range(NT):
-                flip(h0raw[:, t, :].bitcast(F32), ghw, t * P)
-            nc.vector.quantize_mx(
-                out=hcod[:].rearrange("p g c -> p (g c)").bitcast(FP8X4),
-                scales=hscl[:].rearrange("p g c -> p (g c)"),
-                in_=grouped_h[:].rearrange("p g c -> p (g c)"),
-            )
-            step(0)
-            cps = psum.tile([P, P], BF16, name="cps", tag="misc", bufs=2)
-            nc.tensor.transpose(cps[:], colsrc[:], ident_b[:])
-            nc.scalar.copy(out=bcols[:], in_=cps[:, 0:2 * NJ])
-            nc.vector.tensor_tensor(
-                out=bsum_col[:], in0=bcols[:, 0:NJ], in1=bcols[:, NJ:2 * NJ], op=ALU.add
+        def leave(c, t):
+            nc.scalar.activation(
+                out=r_sb[t][:, c * CH:(c + 1) * CH], in_=mm_tiles[(c, t)][:], func=ACT.Copy,
+                accum_out=rsum[:, t, c:c + 1],
             )
 
-        with tc.tile_pool(name="tmpb", bufs=1) as tmpb:
-            w_nat = tmpb.tile([P, NJ, VPAD], BF16, name="w_nat")
-            nc.vector.memset(w_nat[:, :, V:V + 2], 1.0)
-            nc.gpsimd.dma_start(out=w_nat[:, :, 0:V], in_=w_ih1.rearrange("(j p) v -> p j v", p=P))
-            wi_bc = tmpb.tile([P, G], BF16, name="wi_bc")
-            nc.gpsimd.dma_start(out=wi_bc[:], in_=lni_w1.partition_broadcast(P))
-            nc.gpsimd.dma_start(out=wh_bc[:], in_=lnh_w1.partition_broadcast(P))
-            nc.gpsimd.dma_start(out=lncw_bc[:], in_=lnc_w1.partition_broadcast(P))
-            nc.gpsimd.dma_start(out=lncb_bc[:], in_=lnc_b1.partition_broadcast(P))
-            w_t = tmpb.tile([P, G], BF16, name="w_t")
-            craw = tmpb.tile([P, V + 2], F32, name="craw")
+        def mult_run(m):
+            for t in (2 * (m % 2), 2 * (m % 2) + 1):
+                mult(m // 2, t)
 
-            step(1)
+        def leave_run(m):
+            for t in (2 * (m % 2), 2 * (m % 2) + 1):
+                leave(m // 2, t)
 
-            xps = psum.tile([P, NT, P], BF16, name="xps", tag="misc", bufs=2)
-            for t in range(NT):
-                nc.tensor.transpose(xps[:, t, :], x_nat[:, t, :], ident_b[:])
-            nc.scalar.copy(out=xT[:], in_=xps[:].rearrange("p t b -> p (t b)"))
-            gm = psum.tile([P, V + 2], F32, name="gm", tag="misc", bufs=2)
-            for j in range(NJ):
-                nc.tensor.matmul(
-                    gm[:], lhsT=w_nat[:, j, 0:V], rhs=w_nat[:, j, 0:V + 2],
-                    start=(j == 0), stop=(j == NJ - 1),
-                )
-            nc.scalar.activation(out=craw[:], in_=gm[:], func=ACT.Copy, scale=1.0 / G)
-            for i in range(NCH):
-                wps = psum.tile([P, JT, P], BF16, name="wps", tag="misc", bufs=2)
-                for q in range(JT):
-                    nc.tensor.transpose(wps[:, q, :], w_nat[:, JT * i + q, 0:V], ident_b[:])
-                nc.scalar.copy(
-                    out=w_t[:, i * CH:(i + 1) * CH], in_=wps[:].rearrange("p q g -> p (q g)")
-                )
+        side = {}
 
-            step(2)
-
-            nc.vector.tensor_scalar(
-                out=negwbar[:], in0=craw[:, V:V + 1], scalar1=-1.0, scalar2=None, op0=ALU.mult
-            )
-            nb = psum.tile([P, V], F32, name="nb", tag="misc", bufs=2)
-            nc.tensor.matmul(
-                nb[:], lhsT=negwbar[:, 0:1].to_broadcast([P, P]), rhs=ident_f[:], start=True, stop=True
-            )
+        def fold_w(c):
             nc.vector.scalar_tensor_tensor(
-                out=c_sb[:], in0=nb[:], scalar=craw[:, V:V + 1], in1=craw[:, 0:V],
+                out=wpT[:, c * CH:(c + 1) * CH], in0=side["w_t"][:, c * CH:(c + 1) * CH],
+                scalar=negwbar[:, 0:1], in1=wi_bc[:, c * CH:(c + 1) * CH], op0=ALU.add, op1=ALU.mult,
+            )
+
+        for n in range(NJ // 2):
+            if n in (2, 4, 6, 8):
+                load_w(n // 2 + 3, 1)
+            if n == 2:
+                nc.sync.dma_start(out=wh_bc[:], in_=lnh_w1.partition_broadcast(P))
+            if n == 4:
+                nc.sync.dma_start(out=lncw_bc[:], in_=lnc_w1.partition_broadcast(P))
+                nc.sync.dma_start(out=lncb_bc[:], in_=lnc_b1.partition_broadcast(P))
+            if n == 12:
+                side["c0"] = main.tile([P, NT, H], BF16, name="c0_sb", tag="share_c", bufs=1)
+                nc.sync.dma_start(out=side["c0"][:], in_=c0.rearrange("(t p) k -> p t k", p=P))
+
+            widen(2 * n)
+            if n == 3:
+                nc.vector.quantize_mx(
+                    out=hcod[:].rearrange("p g c -> p (g c)").bitcast(FP8X4),
+                    scales=hscl[:].rearrange("p g c -> p (g c)"),
+                    in_=grouped_h[:].rearrange("p g c -> p (g c)"),
+                )
+            if n == 4:
+                nc.vector.tensor_tensor(
+                    out=bsum_col[:], in0=bcols[:, 0:NJ], in1=bcols[:, NJ:2 * NJ], op=ALU.add
+                )
+            if n == 9:
+                nc.vector.tensor_scalar(
+                    out=negwbar[:], in0=craw[:, V:V + 1], scalar1=-1.0, scalar2=None, op0=ALU.mult
+                )
+            if n == 10:
+                nc.vector.scalar_tensor_tensor(
+                    out=c_sb[:], in0=side["nb"][:], scalar=craw[:, V:V + 1], in1=craw[:, 0:V],
+                    op0=ALU.mult, op1=ALU.add,
+                )
+            if n == 11:
+                nc.vector.tensor_tensor(out=ysc[:], in0=side["yp"][:], in1=x_nat[:], op=ALU.mult)
+            if n == 12:
+                nc.vector.tensor_scalar(out=vae[:], in0=va[:], scalar1=EPS, scalar2=None, op0=ALU.add)
+                nc.gpsimd.tensor_tensor(out=a_a[:], in0=vae[:], in1=neg_half[:], op=ALU.pow)
+            widen(2 * n + 1)
+            if n == 11:
+                nc.vector.tensor_reduce(out=va[:], in_=ysc[:], axis=AX.X, op=ALU.add)
+            if n >= 2 and n % 2 == 0:
+                quant_w((n - 2) // 2)
+
+            turn_w(2 * n)
+            turn_w(2 * n + 1)
+            if n == 3:
+                xps = bank([P, NT, P], BF16, "misc")
+                for t in range(NT):
+                    nc.tensor.transpose(xps[:, t, :], x_nat[:, t, :], ident_b[:])
+                cps = bank([P, P], BF16, "gm")
+                nc.tensor.transpose(cps[:], colsrc[:], ident_b[:])
+            if 4 <= n < 12:
+                wps = bank([P, JT, P], BF16, "misc")
+                for q in range(JT):
+                    nc.tensor.transpose(wps[:, q, :], w_nat[:, JT * (n - 4) + q, 0:V], ident_b[:])
+            if n == 14:
+                xsps = bank([P, NT, P], F32, "misc")
+                for t in range(NT):
+                    nc.tensor.transpose(xsps[:, t, :], xs[:, t, :], ident_f[:])
+            if n == 9:
+                side["nb"] = bank([P, V], F32, "gm")
+                nc.tensor.matmul(
+                    side["nb"][:], lhsT=negwbar[:, 0:1].to_broadcast([P, P]), rhs=ident_f[:],
+                    start=True, stop=True,
+                )
+            if n == 10:
+                side["yp"] = bank([P, NT, V], F32, "gm")
+                for t in range(NT):
+                    nc.tensor.matmul(
+                        side["yp"][:, t, :], lhsT=xT[:, t * P:(t + 1) * P], rhs=c_sb[:], start=True, stop=True
+                    )
+            if n >= 3:
+                mult_run(n - 3)
+            if 4 <= n < 8:
+                if n == 4:
+                    side["gm"] = bank([P, V + 2], F32, "gm")
+                for j in range(8 * (n - 4), 8 * (n - 3)):
+                    nc.tensor.matmul(
+                        side["gm"][:], lhsT=w_nat[:, j, 0:V], rhs=w_nat[:, j, 0:V + 2],
+                        start=(j == 0), stop=(j == NJ - 1),
+                    )
+
+            if n == 8:
+                nc.scalar.activation(out=craw[:], in_=side["gm"][:], func=ACT.Copy, scale=1.0 / G)
+            copy_w(2 * n)
+            copy_w(2 * n + 1)
+            if n == 3:
+                nc.scalar.copy(out=xT[:], in_=xps[:].rearrange("p t b -> p (t b)"))
+                nc.scalar.copy(out=bcols[:], in_=cps[:, 0:2 * NJ])
+            if 4 <= n < 12:
+                if n == 4:
+                    side["w_t"] = main.tile([P, G], BF16, name="w_t", tag="share_b", bufs=1, align_bytes=64)
+                nc.scalar.copy(
+                    out=side["w_t"][:, (n - 4) * CH:(n - 3) * CH], in_=wps[:].rearrange("p q g -> p (q g)")
+                )
+            if n == 13:
+                for t in range(NT):
+                    nc.scalar.activation(
+                        out=xs[:, t, :], in_=x_nat[:, t, :], func=ACT.Copy, scale=a_a[:, t:t + 1]
+                    )
+            if n == 14:
+                nc.scalar.copy(out=xsT[:], in_=xsps[:].rearrange("p t b -> p (t b)"))
+            if n >= 3:
+                leave_run(n - 3)
+            if n == 2:
+                for t in range(NT):
+                    turn(("h", t), h0raw[:, t, :].bitcast(F32))
+                    copy_out(("h", t), grouped_h, t * P)
+
+        for c in range(0, 4):
+            fold_w(c)
+        quant_w(NCH - 1)
+        for c in range(4, NCH):
+            fold_w(c)
+        for m in (13, 14, 15):
+            mult_run(m)
+            leave_run(m)
+
+        dps_tiles = {}
+
+        def input_side(i):
+            t, c = i // NCH, i % NCH
+            dps = bank([P, CH], F32, BANKS[c])
+            nc.tensor.matmul(
+                dps[:], lhsT=xsT[:, t * P:(t + 1) * P], rhs=wpT[:, c * CH:(c + 1) * CH],
+                start=True, stop=False,
+            )
+            for q in range(JT):
+                nc.tensor.matmul(
+                    dps[:, q * P:(q + 1) * P],
+                    lhsT=bsum_col[:, JT * c + q:JT * c + q + 1].to_broadcast([P, P]), rhs=ident_f[:],
+                    is_transpose=True, start=False, stop=(q == JT - 1),
+                )
+            dps_tiles[i] = dps
+
+        def var_r(t):
+            junk = main.tile([P, G], BF16, name="junk", tag="share_a", bufs=1)
+            nc.scalar.activation(
+                out=junk[:], in_=r_sb[t][:], func=ACT.Square, bias=negmu[:, t:t + 1], scale=1.0,
+                accum_out=rvs[:, t:t + 1],
+            )
+
+        def rstd_r(t):
+            nc.vector.tensor_scalar(
+                out=rve[:, t:t + 1], in0=rvs[:, t:t + 1], scalar1=1.0 / G, scalar2=EPS,
                 op0=ALU.mult, op1=ALU.add,
             )
+            nc.gpsimd.tensor_tensor(
+                out=a_r[:, t:t + 1], in0=rve[:, t:t + 1], in1=neg_half[:, 0:1], op=ALU.pow
+            )
 
-            step(3)
-
+        def gain_r(t, half):
+            cols = slice(half * (G // 2), (half + 1) * (G // 2))
             nc.vector.scalar_tensor_tensor(
-                out=wpT[:], in0=w_t[:], scalar=negwbar[:, 0:1], in1=wi_bc[:],
+                out=g_sb[t][:, cols], in0=r_sb[t][:, cols], scalar=negmu[:, t:t + 1], in1=wh_bc[:, cols],
                 op0=ALU.add, op1=ALU.mult,
             )
-            for t in range(NT):
-                yp = psum.tile([P, V], F32, name="yp", tag="misc", bufs=2)
-                nc.tensor.matmul(yp[:], lhsT=xT[:, t * P:(t + 1) * P], rhs=c_sb[:], start=True, stop=True)
-                ysc = tmpb.tile([P, V], F32, name="ysc", tag="ysc", bufs=2)
+
+        def gates(t, small):
+            gt = g_sb[t]
+            for c in range(NCH):
                 nc.vector.scalar_tensor_tensor(
-                    out=ysc[:], in0=yp[:], scalar=1.0, in1=x_nat[:, t, :],
-                    op0=ALU.mult, op1=ALU.mult, accum_out=va[:, t:t + 1],
+                    out=gt[:, c * CH:(c + 1) * CH], in0=gt[:, c * CH:(c + 1) * CH],
+                    scalar=a_r[:, t:t + 1], in1=dps_tiles[NCH * t + c][:], op0=ALU.mult, op1=ALU.add,
                 )
-            nc.vector.tensor_scalar(out=vae[:], in0=va[:], scalar1=EPS, scalar2=None, op0=ALU.add)
-            nc.gpsimd.tensor_tensor(out=a_a[:], in0=vae[:], in1=neg_half[:], op=ALU.pow)
+                if t + 1 < NT:
+                    input_side(NCH * (t + 1) + c)
+                if c == 3:
+                    nc.scalar.activation(out=gt[:, 0:2 * H], in_=gt[:, 0:2 * H], func=ACT.Sigmoid)
+                    if small is not None:
+                        small()
+                if c == 5:
+                    nc.scalar.activation(out=gt[:, 2 * H:3 * H], in_=gt[:, 2 * H:3 * H], func=ACT.Tanh)
+                if c == 7:
+                    nc.scalar.activation(out=gt[:, 3 * H:4 * H], in_=gt[:, 3 * H:4 * H], func=ACT.Sigmoid)
 
-            step(4)
+        def s_i(t):
+            return g_sb[t][:, 0:H]
 
-            for t in range(NT):
-                nc.scalar.activation(
-                    out=xs[:, t, :], in_=x_nat[:, t, :], func=ACT.Copy, scale=a_a[:, t:t + 1]
-                )
-            xsps = psum.tile([P, NT, P], F32, name="xsps", tag="misc", bufs=2)
-            for t in range(NT):
-                nc.tensor.transpose(xsps[:, t, :], xs[:, t, :], ident_f[:])
-            nc.scalar.copy(out=xsT[:], in_=xsps[:].rearrange("p t b -> p (t b)"))
+        def s_f(t):
+            return g_sb[t][:, H:2 * H]
 
-        with tc.tile_pool(name="late", bufs=1) as late:
-            step(5)
-            c0_tiles = []
-            for t in range(NT):
-                c0t = late.tile([P, H], BF16, name="c0t%d" % t)
-                nc.sync.dma_start(out=c0t[:], in_=c0[t * P:(t + 1) * P, :])
-                c0_tiles.append(c0t)
-            for c in range(6, NCH + 1):
-                step(c)
+        def t_g(t):
+            return g_sb[t][:, 2 * H:3 * H]
 
-            def stats_r(t):
-                nc.vector.tensor_reduce(out=rtot[:, t:t + 1], in_=rsum[:, t, :], axis=AX.X, op=ALU.add)
-                nc.vector.tensor_scalar(
-                    out=negmu[:, t:t + 1], in0=rtot[:, t:t + 1], scalar1=-1.0 / G, scalar2=None,
-                    op0=ALU.mult,
-                )
+        def s_o(t):
+            return g_sb[t][:, 3 * H:4 * H]
 
-            def var_r(t):
-                junk = late.tile([P, G], BF16, name="junk", tag="junk", bufs=1)
-                nc.scalar.activation(
-                    out=junk[:], in_=r_sb[t][:], func=ACT.Square, bias=negmu[:, t:t + 1], scale=1.0,
-                    accum_out=rvs[:, t:t + 1],
-                )
+        def keep(t):
+            nc.vector.tensor_tensor(out=s_f(t), in0=s_f(t), in1=side["c0"][:, t, :], op=ALU.mult)
 
-            def rstd_r(t):
-                nc.vector.tensor_scalar(
-                    out=rve[:, t:t + 1], in0=rvs[:, t:t + 1], scalar1=1.0 / G, scalar2=EPS,
-                    op0=ALU.mult, op1=ALU.add,
-                )
-                nc.gpsimd.tensor_tensor(
-                    out=a_r[:, t:t + 1], in0=rve[:, t:t + 1], in1=neg_half[:, 0:1], op=ALU.pow
-                )
+        def write(t):
+            nc.vector.tensor_tensor(out=s_i(t), in0=s_i(t), in1=t_g(t), op=ALU.mult)
 
-            def gain_r(t):
-                nc.vector.scalar_tensor_tensor(
-                    out=g_sb[t][:], in0=r_sb[t][:], scalar=negmu[:, t:t + 1], in1=wh_bc[:],
-                    op0=ALU.add, op1=ALU.mult,
-                )
+        def state(t):
+            nc.vector.scalar_tensor_tensor(
+                out=t_g(t), in0=s_i(t), scalar=1.0, in1=s_f(t), op0=ALU.mult, op1=ALU.add,
+                accum_out=csum[:, t:t + 1],
+            )
 
-            def gates(t):
-                gt = g_sb[t]
-                for c in range(NCH):
-                    dps = psum.tile([P, CH], F32, name="dps", tag=("mm", "tp")[c % 2], bufs=3)
-                    nc.tensor.matmul(
-                        dps[:], lhsT=xsT[:, t * P:(t + 1) * P], rhs=wpT[:, c * CH:(c + 1) * CH],
-                        start=True, stop=False,
-                    )
-                    for q in range(JT):
-                        nc.tensor.matmul(
-                            dps[:, q * P:(q + 1) * P], lhsT=bsum_col[:, JT * c + q:JT * c + q + 1].to_broadcast([P, P]), rhs=ident_f[:],
-                            is_transpose=True, start=False, stop=(q == JT - 1),
-                        )
-                    nc.vector.scalar_tensor_tensor(
-                        out=gt[:, c * CH:(c + 1) * CH], in0=gt[:, c * CH:(c + 1) * CH],
-                        scalar=a_r[:, t:t + 1], in1=dps[:], op0=ALU.mult, op1=ALU.add,
-                    )
-                    if c == 3:
-                        nc.scalar.activation(out=gt[:, 0:2 * H], in_=gt[:, 0:2 * H], func=ACT.Sigmoid)
-                    if c == 5:
-                        nc.scalar.activation(out=gt[:, 2 * H:3 * H], in_=gt[:, 2 * H:3 * H], func=ACT.Tanh)
-                    if c == 7:
-                        nc.scalar.activation(out=gt[:, 3 * H:4 * H], in_=gt[:, 3 * H:4 * H], func=ACT.Sigmoid)
+        def mean_c(t):
+            nc.vector.tensor_scalar(
+                out=negmuc[:, t:t + 1], in0=csum[:, t:t + 1], scalar1=-1.0 / H, scalar2=None, op0=ALU.mult
+            )
+            junkc = main.tile([P, H], BF16, name="junkc", tag="junkc", bufs=1)
+            nc.scalar.activation(
+                out=junkc[:], in_=t_g(t), func=ACT.Square, bias=negmuc[:, t:t + 1], scale=1.0,
+                accum_out=cvs[:, t:t + 1],
+            )
 
-            def cell(t):
-                gt = g_sb[t]
-                s_i = gt[:, 0:H]
-                s_f = gt[:, H:2 * H]
-                t_g = gt[:, 2 * H:3 * H]
-                nc.vector.tensor_tensor(out=s_f, in0=s_f, in1=c0_tiles[t][:], op=ALU.mult)
-                nc.vector.tensor_tensor(out=s_i, in0=s_i, in1=t_g, op=ALU.mult)
-                nc.vector.scalar_tensor_tensor(
-                    out=t_g, in0=s_i, scalar=1.0, in1=s_f, op0=ALU.mult, op1=ALU.add,
-                    accum_out=csum[:, t:t + 1],
-                )
-                nc.vector.tensor_scalar(
-                    out=negmuc[:, t:t + 1], in0=csum[:, t:t + 1], scalar1=-1.0 / H, scalar2=None,
-                    op0=ALU.mult,
-                )
-                junkc = late.tile([P, H], BF16, name="junkc", tag="junkc", bufs=1)
-                nc.scalar.activation(
-                    out=junkc[:], in_=t_g, func=ACT.Square, bias=negmuc[:, t:t + 1], scale=1.0,
-                    accum_out=cvs[:, t:t + 1],
-                )
-                nc.vector.tensor_scalar(
-                    out=cve[:, t:t + 1], in0=cvs[:, t:t + 1], scalar1=1.0 / H, scalar2=EPS,
-                    op0=ALU.mult, op1=ALU.add,
-                )
-                nc.gpsimd.tensor_tensor(
-                    out=a_c[:, t:t + 1], in0=cve[:, t:t + 1], in1=neg_half[:, 0:1], op=ALU.pow
-                )
+        def rstd_c(t):
+            nc.vector.tensor_scalar(
+                out=cve[:, t:t + 1], in0=cvs[:, t:t + 1], scalar1=1.0 / H, scalar2=EPS,
+                op0=ALU.mult, op1=ALU.add,
+            )
+            nc.gpsimd.tensor_tensor(
+                out=a_c[:, t:t + 1], in0=cve[:, t:t + 1], in1=neg_half[:, 0:1], op=ALU.pow
+            )
 
-            def norm_c(t):
-                gt = g_sb[t]
-                s_i = gt[:, 0:H]
-                s_f = gt[:, H:2 * H]
-                t_g = gt[:, 2 * H:3 * H]
-                nc.vector.scalar_tensor_tensor(
-                    out=s_i, in0=t_g, scalar=negmuc[:, t:t + 1], in1=lncw_bc[:],
-                    op0=ALU.add, op1=ALU.mult,
-                )
-                nc.vector.scalar_tensor_tensor(
-                    out=s_f, in0=s_i, scalar=a_c[:, t:t + 1], in1=lncb_bc[:],
-                    op0=ALU.mult, op1=ALU.add,
-                )
-                nc.sync.dma_start(out=out_1[t * P:(t + 1) * P, :], in_=s_f)
-                nc.scalar.activation(out=s_i, in_=s_f, func=ACT.Tanh)
+        def gain_c(t):
+            nc.vector.scalar_tensor_tensor(
+                out=s_i(t), in0=t_g(t), scalar=negmuc[:, t:t + 1], in1=lncw_bc[:], op0=ALU.add, op1=ALU.mult
+            )
 
-            def hidden(t):
-                gt = g_sb[t]
-                nc.vector.tensor_tensor(
-                    out=gt[:, 2 * H:3 * H], in0=gt[:, 3 * H:4 * H], in1=gt[:, 0:H], op=ALU.mult
-                )
-                nc.sync.dma_start(out=out_0[t * P:(t + 1) * P, :], in_=gt[:, 2 * H:3 * H])
+        def new_c(t, lo, hi):
+            nc.vector.scalar_tensor_tensor(
+                out=s_f(t)[:, lo:hi], in0=s_i(t)[:, lo:hi], scalar=a_c[:, t:t + 1], in1=lncb_bc[:, lo:hi],
+                op0=ALU.mult, op1=ALU.add,
+            )
+            nc.sync.dma_start(out=out_1[t * P:(t + 1) * P, lo:hi], in_=s_f(t)[:, lo:hi])
+            nc.scalar.activation(out=s_i(t)[:, lo:hi], in_=s_f(t)[:, lo:hi], func=ACT.Tanh)
 
-            for t in range(NT):
-                stats_r(t)
-                var_r(t)
-            gain_r(0)
-            rstd_r(0)
-            gain_r(1)
-            rstd_r(1)
-            gates(0)
-            gain_r(2)
-            rstd_r(2)
-            gates(1)
-            cell(0)
-            gain_r(3)
-            rstd_r(3)
-            gates(2)
-            cell(1)
-            norm_c(0)
-            gates(3)
-            cell(2)
-            norm_c(1)
-            hidden(0)
-            cell(3)
-            norm_c(2)
-            hidden(1)
-            norm_c(3)
-            hidden(2)
-            hidden(3)
+        def new_h(t, lo, hi):
+            nc.vector.tensor_tensor(
+                out=t_g(t)[:, lo:hi], in0=s_o(t)[:, lo:hi], in1=s_i(t)[:, lo:hi], op=ALU.mult
+            )
+            nc.sync.dma_start(out=out_0[t * P:(t + 1) * P, lo:hi], in_=t_g(t)[:, lo:hi])
+
+        for i in range(NCH):
+            input_side(i)
+        nc.vector.tensor_reduce(out=rtot[:], in_=rsum[:], axis=AX.X, op=ALU.add)
+        nc.vector.tensor_scalar(out=negmu[:], in0=rtot[:], scalar1=-1.0 / G, scalar2=None, op0=ALU.mult)
+        var_r(0)
+        var_r(1)
+        var_r(2)
+        gain_r(0, 0)
+        gain_r(0, 1)
+        gain_r(1, 0)
+        rstd_r(0)
+        gain_r(1, 1)
+        gates(0, lambda: rstd_r(1))
+        var_r(3)
+        gain_r(2, 0)
+        rstd_r(2)
+        gain_r(2, 1)
+        gates(1, None)
+        keep(0)
+        write(0)
+        gain_r(3, 0)
+        state(0)
+        gain_r(3, 1)
+        mean_c(0)
+        rstd_r(3)
+        gates(2, lambda: rstd_c(0))
+        keep(1)
+        write(1)
+        gain_c(0)
+        state(1)
+        new_c(0, 0, H)
+        mean_c(1)
+        gates(3, lambda: rstd_c(1))
+        keep(2)
+        write(2)
+        gain_c(1)
+        state(2)
+        new_c(1, 0, H)
+        mean_c(2)
+        new_h(0, 0, H)
+        keep(3)
+        rstd_c(2)
+        write(3)
+        gain_c(2)
+        state(3)
+        new_c(2, 0, H)
+        mean_c(3)
+        new_h(1, 0, H)
+        gain_c(3)
+        rstd_c(3)
+        new_h(2, 0, H)
+        new_c(3, 0, H // 2)
+        new_c(3, H // 2, H)
+        new_h(3, 0, H // 2)
+        new_h(3, H // 2, H)

@@ -248,6 +248,8 @@ def tile_multilstm_pa_kernel(
                 quant_w((n - 2) // 2)
 
             turn_w(2 * n)
+            if n >= 3:
+                mult((n - 3) // 2, 2 * ((n - 3) % 2))
             turn_w(2 * n + 1)
             if n == 3:
                 xps = bank([P, NT, P], BF16, "misc")
@@ -276,7 +278,7 @@ def tile_multilstm_pa_kernel(
                         side["yp"][:, t, :], lhsT=xT[:, t * P:(t + 1) * P], rhs=c_sb[:], start=True, stop=True
                     )
             if n >= 3:
-                mult_run(n - 3)
+                mult((n - 3) // 2, 2 * ((n - 3) % 2) + 1)
             if 4 <= n < 8:
                 if n == 4:
                     side["gm"] = bank([P, V + 2], F32, "gm")
@@ -289,6 +291,8 @@ def tile_multilstm_pa_kernel(
             if n == 8:
                 nc.scalar.activation(out=craw[:], in_=side["gm"][:], func=ACT.Copy, scale=1.0 / G)
             copy_w(2 * n)
+            if n >= 3:
+                leave((n - 3) // 2, 2 * ((n - 3) % 2))
             copy_w(2 * n + 1)
             if n == 3:
                 nc.scalar.copy(out=xT[:], in_=xps[:].rearrange("p t b -> p (t b)"))
@@ -307,7 +311,7 @@ def tile_multilstm_pa_kernel(
             if n == 14:
                 nc.scalar.copy(out=xsT[:], in_=xsps[:].rearrange("p t b -> p (t b)"))
             if n >= 3:
-                leave_run(n - 3)
+                leave((n - 3) // 2, 2 * ((n - 3) % 2) + 1)
             if n == 2:
                 for t in range(NT):
                     turn(("h", t), h0raw[:, t, :].bitcast(F32))

@@ -326,22 +326,26 @@ def tile_multilstm_pa_kernel(
             mult_run(m)
             leave_run(m)
 
+        order = [(t, c) for t in range(NT) for c in range(6)] + [(t, c) for t in range(NT) for c in (6, 7)]
         dps_tiles = {}
 
-        def input_side(i):
-            t, c = i // NCH, i % NCH
-            dps = bank([P, CH], F32, BANKS[c])
-            nc.tensor.matmul(
-                dps[:], lhsT=xsT[:, t * P:(t + 1) * P], rhs=wpT[:, c * CH:(c + 1) * CH],
-                start=True, stop=False,
-            )
-            for q in range(JT):
+        def input_side(q):
+            four = range(4 * q, 4 * q + 4)
+            for i in four:
+                t, c = order[i]
+                dps_tiles[i] = bank([P, CH], F32, BANKS[i % 8])
                 nc.tensor.matmul(
-                    dps[:, q * P:(q + 1) * P],
-                    lhsT=bsum_col[:, JT * c + q:JT * c + q + 1].to_broadcast([P, P]), rhs=ident_f[:],
-                    is_transpose=True, start=False, stop=(q == JT - 1),
+                    dps_tiles[i][:], lhsT=xsT[:, t * P:(t + 1) * P], rhs=wpT[:, c * CH:(c + 1) * CH],
+                    start=True, stop=False,
                 )
-            dps_tiles[i] = dps
+            for i in four:
+                t, c = order[i]
+                for q4 in range(JT):
+                    nc.tensor.matmul(
+                        dps_tiles[i][:, q4 * P:(q4 + 1) * P],
+                        lhsT=bsum_col[:, JT * c + q4:JT * c + q4 + 1].to_broadcast([P, P]), rhs=ident_f[:],
+                        is_transpose=True, start=False, stop=(q4 == JT - 1),
+                    )
 
         def var_r(t):
             junk = main.tile([P, G], BF16, name="junk", tag="share_a", bufs=1)
@@ -349,40 +353,33 @@ def tile_multilstm_pa_kernel(
                 out=junk[:], in_=r_sb[t][:], func=ACT.Square, bias=negmu[:, t:t + 1], scale=1.0,
                 accum_out=rvs[:, t:t + 1],
             )
-
-        def rstd_r(t):
-            nc.vector.tensor_scalar(
-                out=rve[:, t:t + 1], in0=rvs[:, t:t + 1], scalar1=1.0 / G, scalar2=EPS,
-                op0=ALU.mult, op1=ALU.add,
+            nc.scalar.activation(
+                out=rve[:, t:t + 1], in_=rvs[:, t:t + 1], func=ACT.Copy, scale=1.0 / G, bias=EPS
             )
             nc.gpsimd.tensor_tensor(
                 out=a_r[:, t:t + 1], in0=rve[:, t:t + 1], in1=neg_half[:, 0:1], op=ALU.pow
             )
 
-        def gain_r(t, half):
-            cols = slice(half * (G // 2), (half + 1) * (G // 2))
+        def gain_r(t, part):
+            cols = slice(part * H, (part + 1) * H)
             nc.vector.scalar_tensor_tensor(
                 out=g_sb[t][:, cols], in0=r_sb[t][:, cols], scalar=negmu[:, t:t + 1], in1=wh_bc[:, cols],
                 op0=ALU.add, op1=ALU.mult,
             )
 
-        def gates(t, small):
+        def gate(i):
+            t, c = order[i]
             gt = g_sb[t]
-            for c in range(NCH):
-                nc.vector.scalar_tensor_tensor(
-                    out=gt[:, c * CH:(c + 1) * CH], in0=gt[:, c * CH:(c + 1) * CH],
-                    scalar=a_r[:, t:t + 1], in1=dps_tiles[NCH * t + c][:], op0=ALU.mult, op1=ALU.add,
-                )
-                if t + 1 < NT:
-                    input_side(NCH * (t + 1) + c)
-                if c == 3:
-                    nc.scalar.activation(out=gt[:, 0:2 * H], in_=gt[:, 0:2 * H], func=ACT.Sigmoid)
-                    if small is not None:
-                        small()
-                if c == 5:
-                    nc.scalar.activation(out=gt[:, 2 * H:3 * H], in_=gt[:, 2 * H:3 * H], func=ACT.Tanh)
-                if c == 7:
-                    nc.scalar.activation(out=gt[:, 3 * H:4 * H], in_=gt[:, 3 * H:4 * H], func=ACT.Sigmoid)
+            nc.vector.scalar_tensor_tensor(
+                out=gt[:, c * CH:(c + 1) * CH], in0=gt[:, c * CH:(c + 1) * CH],
+                scalar=a_r[:, t:t + 1], in1=dps_tiles[i][:], op0=ALU.mult, op1=ALU.add,
+            )
+            if c == 3:
+                nc.scalar.activation(out=gt[:, 0:2 * H], in_=gt[:, 0:2 * H], func=ACT.Sigmoid)
+            if c == 5:
+                nc.scalar.activation(out=gt[:, 2 * H:3 * H], in_=gt[:, 2 * H:3 * H], func=ACT.Tanh)
+            if c == 7:
+                nc.scalar.activation(out=gt[:, 3 * H:4 * H], in_=gt[:, 3 * H:4 * H], func=ACT.Sigmoid)
 
         def s_i(t):
             return g_sb[t][:, 0:H]
@@ -408,7 +405,7 @@ def tile_multilstm_pa_kernel(
                 accum_out=csum[:, t:t + 1],
             )
 
-        def mean_c(t):
+        def stats_c(t):
             nc.vector.tensor_scalar(
                 out=negmuc[:, t:t + 1], in0=csum[:, t:t + 1], scalar1=-1.0 / H, scalar2=None, op0=ALU.mult
             )
@@ -417,11 +414,8 @@ def tile_multilstm_pa_kernel(
                 out=junkc[:], in_=t_g(t), func=ACT.Square, bias=negmuc[:, t:t + 1], scale=1.0,
                 accum_out=cvs[:, t:t + 1],
             )
-
-        def rstd_c(t):
-            nc.vector.tensor_scalar(
-                out=cve[:, t:t + 1], in0=cvs[:, t:t + 1], scalar1=1.0 / H, scalar2=EPS,
-                op0=ALU.mult, op1=ALU.add,
+            nc.scalar.activation(
+                out=cve[:, t:t + 1], in_=cvs[:, t:t + 1], func=ACT.Copy, scale=1.0 / H, bias=EPS
             )
             nc.gpsimd.tensor_tensor(
                 out=a_c[:, t:t + 1], in0=cve[:, t:t + 1], in1=neg_half[:, 0:1], op=ALU.pow
@@ -432,13 +426,12 @@ def tile_multilstm_pa_kernel(
                 out=s_i(t), in0=t_g(t), scalar=negmuc[:, t:t + 1], in1=lncw_bc[:], op0=ALU.add, op1=ALU.mult
             )
 
-        def new_c(t, lo, hi):
+        def new_c(t):
             nc.vector.scalar_tensor_tensor(
-                out=s_f(t)[:, lo:hi], in0=s_i(t)[:, lo:hi], scalar=a_c[:, t:t + 1], in1=lncb_bc[:, lo:hi],
-                op0=ALU.mult, op1=ALU.add,
+                out=s_f(t), in0=s_i(t), scalar=a_c[:, t:t + 1], in1=lncb_bc[:], op0=ALU.mult, op1=ALU.add
             )
-            nc.sync.dma_start(out=out_1[t * P:(t + 1) * P, lo:hi], in_=s_f(t)[:, lo:hi])
-            nc.scalar.activation(out=s_i(t)[:, lo:hi], in_=s_f(t)[:, lo:hi], func=ACT.Tanh)
+            nc.sync.dma_start(out=out_1[t * P:(t + 1) * P, :], in_=s_f(t))
+            nc.scalar.activation(out=s_i(t), in_=s_f(t), func=ACT.Tanh)
 
         def new_h(t, lo, hi):
             nc.vector.tensor_tensor(
@@ -446,58 +439,37 @@ def tile_multilstm_pa_kernel(
             )
             nc.sync.dma_start(out=out_0[t * P:(t + 1) * P, lo:hi], in_=t_g(t)[:, lo:hi])
 
-        for i in range(NCH):
-            input_side(i)
+        gains = [(gain_r, t, part) for t in range(NT) for part in range(4)]
+        first = gains[0:6]
+        steps = gains[6:]
+        for t in range(NT):
+            if t > 0:
+                steps.append((gain_c, t - 1))
+            steps.extend([(keep, t), (write, t), (state, t)])
+            if t > 0:
+                steps.append((new_c, t - 1))
+        steps.extend([
+            (gain_c, 3), (new_h, 0, 0, H), (new_h, 1, 0, H), (new_c, 3), (new_h, 2, 0, H),
+            (new_h, 3, 0, H // 2), (new_h, 3, H // 2, H),
+        ])
+
+        input_side(0)
+        input_side(1)
         nc.vector.tensor_reduce(out=rtot[:], in_=rsum[:], axis=AX.X, op=ALU.add)
         nc.vector.tensor_scalar(out=negmu[:], in0=rtot[:], scalar1=-1.0 / G, scalar2=None, op0=ALU.mult)
-        var_r(0)
-        var_r(1)
-        var_r(2)
-        gain_r(0, 0)
-        gain_r(0, 1)
-        gain_r(1, 0)
-        rstd_r(0)
-        gain_r(1, 1)
-        gates(0, lambda: rstd_r(1))
-        var_r(3)
-        gain_r(2, 0)
-        rstd_r(2)
-        gain_r(2, 1)
-        gates(1, None)
-        keep(0)
-        write(0)
-        gain_r(3, 0)
-        state(0)
-        gain_r(3, 1)
-        mean_c(0)
-        rstd_r(3)
-        gates(2, lambda: rstd_c(0))
-        keep(1)
-        write(1)
-        gain_c(0)
-        state(1)
-        new_c(0, 0, H)
-        mean_c(1)
-        gates(3, lambda: rstd_c(1))
-        keep(2)
-        write(2)
-        gain_c(1)
-        state(2)
-        new_c(1, 0, H)
-        mean_c(2)
-        new_h(0, 0, H)
-        keep(3)
-        rstd_c(2)
-        write(3)
-        gain_c(2)
-        state(3)
-        new_c(2, 0, H)
-        mean_c(3)
-        new_h(1, 0, H)
-        gain_c(3)
-        rstd_c(3)
-        new_h(2, 0, H)
-        new_c(3, 0, H // 2)
-        new_c(3, H // 2, H)
-        new_h(3, 0, H // 2)
-        new_h(3, H // 2, H)
+        for t in range(3):
+            var_r(t)
+        for step in first:
+            step[0](*step[1:])
+        last = None
+        for n, step in enumerate(steps):
+            if n < len(order):
+                gate(n)
+                if n % 4 == 3 and n // 4 + 2 < len(order) // 4:
+                    input_side(n // 4 + 2)
+                if n == 5:
+                    var_r(3)
+            if last is not None and last[0] is state:
+                stats_c(last[1])
+            step[0](*step[1:])
+            last = step

@@ -24,6 +24,7 @@ CH = 512
 NCH = G // CH
 JT = CH // P
 NJ = G // P
+LAG = 3
 VPAD = 144
 BANKS = ("tp", "mm", "gm", "tp", "mm", "misc", "tp", "mm")
 BUFS = {"tp": 3, "mm": 3, "gm": 1, "misc": 1}
@@ -62,7 +63,7 @@ def tile_multilstm_pa_kernel(
         r_sb = ring[0:NT]
         g_sb = [ring[NT]] + ring[0:NT - 1]
         rsum = main.tile([P, NT, NCH], F32, name="rsum")
-        rtot = main.tile([P, NT], F32, name="rtot")
+        rtot = main.tile([P, NT, NCH], F32, name="rtot")
         negmu = main.tile([P, NT], F32, name="negmu")
         rvs = main.tile([P, NT], F32, name="rvs")
         rve = main.tile([P, NT], F32, name="rve")
@@ -98,10 +99,21 @@ def tile_multilstm_pa_kernel(
                 )
             wb_tiles[c] = wb
 
-        nc.sync.dma_start(
-            out=scale_bc[:], in_=w_hh1_scale.rearrange("o k -> (o k)").partition_broadcast(P)
-        )
-        load_w(0, JT)
+        def load_scale(i):
+            cols = slice(i * (H // 4), (i + 1) * (H // 4))
+            nc.sync.dma_start(
+                out=scale_bc[:, cols], in_=w_hh1_scale[:, cols].rearrange("o k -> (o k)").partition_broadcast(P)
+            )
+
+        wb0 = main.tile([P, JT, H], U8, name="wb", tag="wb", bufs=4)
+        wb_tiles[0] = wb0
+        src0 = w_hh1_bytes[0:CH, :].rearrange("(j p) k -> p j k", p=P)
+        load_scale(0)
+        nc.sync.dma_start(out=wb0[:, 0:1, :], in_=src0[:, 0:1, :])
+        for i in range(1, 4):
+            load_scale(i)
+        for j in range(1, JT):
+            nc.sync.dma_start(out=wb0[:, j:j + 1, :], in_=src0[:, j:j + 1, :])
         load_w(1, 1)
         nc.sync.dma_start(out=h0raw[:], in_=h0.rearrange("(t p) k -> p t k", p=P))
         nc.vector.memset(neg_half[:], -0.5)
@@ -126,9 +138,13 @@ def tile_multilstm_pa_kernel(
 
         def widen(k):
             wbf = main.tile([P, H], BF16, name="wbf", tag="wbf", bufs=6)
-            nc.vector.tensor_tensor(
-                out=wbf[:], in0=wb_tiles[k // JT][:, k % JT, :].bitcast(FP8), in1=scale_bc[:], op=ALU.mult
-            )
+            pieces = 4 if k == 0 else 1
+            for i in range(pieces):
+                cols = slice(i * (H // pieces), (i + 1) * (H // pieces))
+                nc.vector.tensor_tensor(
+                    out=wbf[:, cols], in0=wb_tiles[k // JT][:, k % JT, cols].bitcast(FP8), in1=scale_bc[:, cols],
+                    op=ALU.mult,
+                )
             wbf_tiles[k] = wbf
 
         def turn(key, words):
@@ -187,6 +203,11 @@ def tile_multilstm_pa_kernel(
                 out=r_sb[t][:, c * CH:(c + 1) * CH], in_=mm_tiles[(c, t)][:], func=ACT.Copy,
                 accum_out=rsum[:, t, c:c + 1],
             )
+            if c == NCH - 1:
+                nc.scalar.activation(
+                    out=rtot[:, t, :], in_=rsum[:, t, :], func=ACT.Copy, scale=-1.0 / G,
+                    accum_out=negmu[:, t:t + 1],
+                )
 
         def mult_run(m):
             for t in (2 * (m % 2), 2 * (m % 2) + 1):
@@ -198,10 +219,10 @@ def tile_multilstm_pa_kernel(
 
         side = {}
 
-        def fold_w(c):
+        def fold_w(lo, hi):
             nc.vector.scalar_tensor_tensor(
-                out=wpT[:, c * CH:(c + 1) * CH], in0=side["w_t"][:, c * CH:(c + 1) * CH],
-                scalar=negwbar[:, 0:1], in1=wi_bc[:, c * CH:(c + 1) * CH], op0=ALU.add, op1=ALU.mult,
+                out=wpT[:, lo:hi], in0=side["w_t"][:, lo:hi], scalar=negwbar[:, 0:1], in1=wi_bc[:, lo:hi],
+                op0=ALU.add, op1=ALU.mult,
             )
 
         for n in range(NJ // 2):
@@ -217,13 +238,7 @@ def tile_multilstm_pa_kernel(
                 nc.sync.dma_start(out=side["c0"][:], in_=c0.rearrange("(t p) k -> p t k", p=P))
 
             widen(2 * n)
-            if n == 3:
-                nc.vector.quantize_mx(
-                    out=hcod[:].rearrange("p g c -> p (g c)").bitcast(FP8X4),
-                    scales=hscl[:].rearrange("p g c -> p (g c)"),
-                    in_=grouped_h[:].rearrange("p g c -> p (g c)"),
-                )
-            if n == 4:
+            if n == 5:
                 nc.vector.tensor_tensor(
                     out=bsum_col[:], in0=bcols[:, 0:NJ], in1=bcols[:, NJ:2 * NJ], op=ALU.add
                 )
@@ -231,25 +246,31 @@ def tile_multilstm_pa_kernel(
                 nc.vector.tensor_scalar(
                     out=negwbar[:], in0=craw[:, V:V + 1], scalar1=-1.0, scalar2=None, op0=ALU.mult
                 )
-            if n == 10:
+            if n == 11:
                 nc.vector.scalar_tensor_tensor(
                     out=c_sb[:], in0=side["nb"][:], scalar=craw[:, V:V + 1], in1=craw[:, 0:V],
                     op0=ALU.mult, op1=ALU.add,
                 )
-            if n == 11:
-                nc.vector.tensor_tensor(out=ysc[:], in0=side["yp"][:], in1=x_nat[:], op=ALU.mult)
+            if n == 13:
+                nc.vector.tensor_reduce(out=va[:], in_=ysc[:], axis=AX.X, op=ALU.add)
+            widen(2 * n + 1)
+            if n == 3:
+                nc.vector.quantize_mx(
+                    out=hcod[:].rearrange("p g c -> p (g c)").bitcast(FP8X4),
+                    scales=hscl[:].rearrange("p g c -> p (g c)"),
+                    in_=grouped_h[:].rearrange("p g c -> p (g c)"),
+                )
             if n == 12:
+                nc.vector.tensor_tensor(out=ysc[:], in0=side["yp"][:], in1=x_nat[:], op=ALU.mult)
+            if n == 13:
                 nc.vector.tensor_scalar(out=vae[:], in0=va[:], scalar1=EPS, scalar2=None, op0=ALU.add)
                 nc.gpsimd.tensor_tensor(out=a_a[:], in0=vae[:], in1=neg_half[:], op=ALU.pow)
-            widen(2 * n + 1)
-            if n == 11:
-                nc.vector.tensor_reduce(out=va[:], in_=ysc[:], axis=AX.X, op=ALU.add)
             if n >= 2 and n % 2 == 0:
                 quant_w((n - 2) // 2)
 
             turn_w(2 * n)
-            if n >= 3:
-                mult((n - 3) // 2, 2 * ((n - 3) % 2))
+            if n >= LAG:
+                mult((n - LAG) // 2, 2 * ((n - LAG) % 2))
             turn_w(2 * n + 1)
             if n == 3:
                 xps = bank([P, NT, P], BF16, "misc")
@@ -261,7 +282,7 @@ def tile_multilstm_pa_kernel(
                 wps = bank([P, JT, P], BF16, "misc")
                 for q in range(JT):
                     nc.tensor.transpose(wps[:, q, :], w_nat[:, JT * (n - 4) + q, 0:V], ident_b[:])
-            if n == 14:
+            if n == 15:
                 xsps = bank([P, NT, P], F32, "misc")
                 for t in range(NT):
                     nc.tensor.transpose(xsps[:, t, :], xs[:, t, :], ident_f[:])
@@ -271,14 +292,14 @@ def tile_multilstm_pa_kernel(
                     side["nb"][:], lhsT=negwbar[:, 0:1].to_broadcast([P, P]), rhs=ident_f[:],
                     start=True, stop=True,
                 )
-            if n == 10:
+            if n == 11:
                 side["yp"] = bank([P, NT, V], F32, "gm")
                 for t in range(NT):
                     nc.tensor.matmul(
                         side["yp"][:, t, :], lhsT=xT[:, t * P:(t + 1) * P], rhs=c_sb[:], start=True, stop=True
                     )
-            if n >= 3:
-                mult((n - 3) // 2, 2 * ((n - 3) % 2) + 1)
+            if n >= LAG:
+                mult((n - LAG) // 2, 2 * ((n - LAG) % 2) + 1)
             if 4 <= n < 8:
                 if n == 4:
                     side["gm"] = bank([P, V + 2], F32, "gm")
@@ -291,8 +312,8 @@ def tile_multilstm_pa_kernel(
             if n == 8:
                 nc.scalar.activation(out=craw[:], in_=side["gm"][:], func=ACT.Copy, scale=1.0 / G)
             copy_w(2 * n)
-            if n >= 3:
-                leave((n - 3) // 2, 2 * ((n - 3) % 2))
+            if n >= LAG:
+                leave((n - LAG) // 2, 2 * ((n - LAG) % 2))
             copy_w(2 * n + 1)
             if n == 3:
                 nc.scalar.copy(out=xT[:], in_=xps[:].rearrange("p t b -> p (t b)"))
@@ -303,28 +324,27 @@ def tile_multilstm_pa_kernel(
                 nc.scalar.copy(
                     out=side["w_t"][:, (n - 4) * CH:(n - 3) * CH], in_=wps[:].rearrange("p q g -> p (q g)")
                 )
-            if n == 13:
+            if n == 14:
                 for t in range(NT):
                     nc.scalar.activation(
                         out=xs[:, t, :], in_=x_nat[:, t, :], func=ACT.Copy, scale=a_a[:, t:t + 1]
                     )
-            if n == 14:
+            if n == 15:
                 nc.scalar.copy(out=xsT[:], in_=xsps[:].rearrange("p t b -> p (t b)"))
-            if n >= 3:
-                leave((n - 3) // 2, 2 * ((n - 3) % 2) + 1)
+            if n >= LAG:
+                leave((n - LAG) // 2, 2 * ((n - LAG) % 2) + 1)
             if n == 2:
                 for t in range(NT):
                     turn(("h", t), h0raw[:, t, :].bitcast(F32))
                     copy_out(("h", t), grouped_h, t * P)
 
-        for c in range(0, 4):
-            fold_w(c)
+        fold_w(0, 3 * CH)
         quant_w(NCH - 1)
-        for c in range(4, NCH):
-            fold_w(c)
-        for m in (13, 14, 15):
+        fold_w(3 * CH, 6 * CH)
+        for m in range(NJ // 2 - LAG, NJ // 2 - 1):
             mult_run(m)
             leave_run(m)
+        mult_run(NJ // 2 - 1)
 
         order = [(t, c) for t in range(NT) for c in range(6)] + [(t, c) for t in range(NT) for c in (6, 7)]
         dps_tiles = {}
@@ -360,8 +380,8 @@ def tile_multilstm_pa_kernel(
                 out=a_r[:, t:t + 1], in0=rve[:, t:t + 1], in1=neg_half[:, 0:1], op=ALU.pow
             )
 
-        def gain_r(t, part):
-            cols = slice(part * H, (part + 1) * H)
+        def gain_r(t, part, parts):
+            cols = slice(part * H, (part + parts) * H)
             nc.vector.scalar_tensor_tensor(
                 out=g_sb[t][:, cols], in0=r_sb[t][:, cols], scalar=negmu[:, t:t + 1], in1=wh_bc[:, cols],
                 op0=ALU.add, op1=ALU.mult,
@@ -439,9 +459,8 @@ def tile_multilstm_pa_kernel(
             )
             nc.sync.dma_start(out=out_0[t * P:(t + 1) * P, lo:hi], in_=t_g(t)[:, lo:hi])
 
-        gains = [(gain_r, t, part) for t in range(NT) for part in range(4)]
-        first = gains[0:6]
-        steps = gains[6:]
+        first = [(gain_r, 0, 0, 4), (fold_w, 6 * CH, G), (gain_r, 1, 0, 2)]
+        steps = [(gain_r, 1, 2, 1), (gain_r, 1, 3, 1)] + [(gain_r, t, part, 1) for t in (2, 3) for part in range(4)]
         for t in range(NT):
             if t > 0:
                 steps.append((gain_c, t - 1))
@@ -453,12 +472,12 @@ def tile_multilstm_pa_kernel(
             (new_h, 3, 0, H // 2), (new_h, 3, H // 2, H),
         ])
 
+        var_r(0)
+        leave_run(NJ // 2 - 1)
         input_side(0)
         input_side(1)
-        nc.vector.tensor_reduce(out=rtot[:], in_=rsum[:], axis=AX.X, op=ALU.add)
-        nc.vector.tensor_scalar(out=negmu[:], in0=rtot[:], scalar1=-1.0 / G, scalar2=None, op0=ALU.mult)
-        for t in range(3):
-            var_r(t)
+        var_r(1)
+        var_r(2)
         for step in first:
             step[0](*step[1:])
         last = None

@@ -99,21 +99,10 @@ def tile_multilstm_pa_kernel(
                 )
             wb_tiles[c] = wb
 
-        def load_scale(i):
-            cols = slice(i * (H // 4), (i + 1) * (H // 4))
-            nc.sync.dma_start(
-                out=scale_bc[:, cols], in_=w_hh1_scale[:, cols].rearrange("o k -> (o k)").partition_broadcast(P)
-            )
-
-        wb0 = main.tile([P, JT, H], U8, name="wb", tag="wb", bufs=4)
-        wb_tiles[0] = wb0
-        src0 = w_hh1_bytes[0:CH, :].rearrange("(j p) k -> p j k", p=P)
-        load_scale(0)
-        nc.sync.dma_start(out=wb0[:, 0:1, :], in_=src0[:, 0:1, :])
-        for i in range(1, 4):
-            load_scale(i)
-        for j in range(1, JT):
-            nc.sync.dma_start(out=wb0[:, j:j + 1, :], in_=src0[:, j:j + 1, :])
+        nc.sync.dma_start(
+            out=scale_bc[:], in_=w_hh1_scale.rearrange("o k -> (o k)").partition_broadcast(P)
+        )
+        load_w(0, JT)
         load_w(1, 1)
         nc.sync.dma_start(out=h0raw[:], in_=h0.rearrange("(t p) k -> p t k", p=P))
         nc.vector.memset(neg_half[:], -0.5)
@@ -138,13 +127,9 @@ def tile_multilstm_pa_kernel(
 
         def widen(k):
             wbf = main.tile([P, H], BF16, name="wbf", tag="wbf", bufs=6)
-            pieces = 4 if k == 0 else 1
-            for i in range(pieces):
-                cols = slice(i * (H // pieces), (i + 1) * (H // pieces))
-                nc.vector.tensor_tensor(
-                    out=wbf[:, cols], in0=wb_tiles[k // JT][:, k % JT, cols].bitcast(FP8), in1=scale_bc[:, cols],
-                    op=ALU.mult,
-                )
+            nc.vector.tensor_tensor(
+                out=wbf[:], in0=wb_tiles[k // JT][:, k % JT, :].bitcast(FP8), in1=scale_bc[:], op=ALU.mult
+            )
             wbf_tiles[k] = wbf
 
         def turn(key, words):

@@ -253,8 +253,9 @@ def tile_multilstm_pa_kernel(
             if n >= 2 and n % 2 == 0:
                 quant_w((n - 2) // 2)
 
+            split = n % 2 == 1 and n > LAG
             turn_w(2 * n)
-            if n >= LAG:
+            if n >= LAG and split:
                 mult((n - LAG) // 2, 2 * ((n - LAG) % 2))
             turn_w(2 * n + 1)
             if n == 3:
@@ -283,6 +284,8 @@ def tile_multilstm_pa_kernel(
                     nc.tensor.matmul(
                         side["yp"][:, t, :], lhsT=xT[:, t * P:(t + 1) * P], rhs=c_sb[:], start=True, stop=True
                     )
+            if n >= LAG and not split:
+                mult((n - LAG) // 2, 2 * ((n - LAG) % 2))
             if n >= LAG:
                 mult((n - LAG) // 2, 2 * ((n - LAG) % 2) + 1)
             if 4 <= n < 8:
@@ -297,7 +300,7 @@ def tile_multilstm_pa_kernel(
             if n == 8:
                 nc.scalar.activation(out=craw[:], in_=side["gm"][:], func=ACT.Copy, scale=1.0 / G)
             copy_w(2 * n)
-            if n >= LAG:
+            if n >= LAG and split:
                 leave((n - LAG) // 2, 2 * ((n - LAG) % 2))
             copy_w(2 * n + 1)
             if n == 3:
@@ -316,6 +319,8 @@ def tile_multilstm_pa_kernel(
                     )
             if n == 15:
                 nc.scalar.copy(out=xsT[:], in_=xsps[:].rearrange("p t b -> p (t b)"))
+            if n >= LAG and not split:
+                leave((n - LAG) // 2, 2 * ((n - LAG) % 2))
             if n >= LAG:
                 leave((n - LAG) // 2, 2 * ((n - LAG) % 2) + 1)
             if n == 2:

@@ -26,7 +26,7 @@ JT = CH // P
 NJ = G // P
 LAG = 3
 VPAD = 144
-BANKS = ("tp", "mm", "gm", "tp", "mm", "misc", "tp", "mm")
+OJ = H // P
 BUFS = {"tp": 3, "mm": 3, "gm": 1, "misc": 1}
 
 
@@ -59,9 +59,9 @@ def tile_multilstm_pa_kernel(
         colsrc = main.tile([P, P], BF16, name="colsrc")
         hcod = main.tile([P, 2, B], U32, name="hcod", align_bytes=64)
         hscl = main.tile([P, 2, B], U8, name="hscl", align_bytes=64)
-        ring = [main.tile([P, G], F32, name="ring%d" % t) for t in range(NT + 1)]
+        ring = [main.tile([P, G], F32, name="ring%d" % t) for t in range(NT + 2)]
         r_sb = ring[0:NT]
-        g_sb = [ring[NT]] + ring[0:NT - 1]
+        g_sb = ring[NT:NT + 2] + ring[0:NT - 2]
         rsum = main.tile([P, NT, NCH], F32, name="rsum")
         rtot = main.tile([P, NT, NCH], F32, name="rtot")
         negmu = main.tile([P, NT], F32, name="negmu")
@@ -77,7 +77,7 @@ def tile_multilstm_pa_kernel(
         cve = main.tile([P, NT], F32, name="cve")
         a_c = main.tile([P, NT], F32, name="a_c")
         negwbar = main.tile([P, 1], F32, name="negwbar")
-        bcols = main.tile([P, 2 * NJ], F32, name="bcols")
+        bcols = main.tile([P, 2 * NJ + OJ], F32, name="bcols")
         bsum_col = main.tile([P, NJ], F32, name="bsum_col")
         neg_half = main.tile([P, NT], F32, name="neg_half")
         warm = main.tile([P, 1], F32, name="warm")
@@ -114,6 +114,7 @@ def tile_multilstm_pa_kernel(
         nc.sync.dma_start(out=x_nat[:], in_=x.rearrange("(t p) v -> p t v", p=P))
         nc.sync.dma_start(out=colsrc[0:NJ, :], in_=lni_b1.rearrange("(j p) -> j p", p=P))
         nc.sync.dma_start(out=colsrc[NJ:2 * NJ, :], in_=lnh_b1.rearrange("(j p) -> j p", p=P))
+        nc.sync.dma_start(out=colsrc[2 * NJ:2 * NJ + OJ, :], in_=lnh_w1[3 * H:4 * H].rearrange("(j p) -> j p", p=P))
         load_w(2, 1)
         nc.sync.dma_start(out=w_nat[:, :, 0:V], in_=w_ih1.rearrange("(j p) v -> p j v", p=P))
         load_w(3, 1)
@@ -305,7 +306,7 @@ def tile_multilstm_pa_kernel(
             copy_w(2 * n + 1)
             if n == 3:
                 nc.scalar.copy(out=xT[:], in_=xps[:].rearrange("p t b -> p (t b)"))
-                nc.scalar.copy(out=bcols[:], in_=cps[:, 0:2 * NJ])
+                nc.scalar.copy(out=bcols[:], in_=cps[:, 0:2 * NJ + OJ])
             if 4 <= n < 12:
                 if n == 4:
                     side["w_t"] = main.tile([P, G], BF16, name="w_t", tag="share_b", bufs=1, align_bytes=64)
@@ -336,19 +337,29 @@ def tile_multilstm_pa_kernel(
             leave_run(m)
         mult_run(NJ // 2 - 1)
 
-        order = [(t, c) for t in range(NT) for c in range(6)] + [(t, c) for t in range(NT) for c in (6, 7)]
-        dps_tiles = {}
+        ops = {}
 
-        def input_side(q):
-            four = range(4 * q, 4 * q + 4)
-            for i in four:
+        def define(name, deps, fn, *args):
+            ops[name] = (deps, fn, args)
+
+        order = [(t, c) for t in range(NT) for c in range(6)]
+        dps_tiles = {}
+        fwd_tiles = {}
+        o_tiles = {}
+        z_t = [
+            main.tile([P, JT, B], F32, name="z_t%d" % half, tag="grouped", bufs=2, align_bytes=64) for half in range(2)
+        ]
+
+        def in_group(k):
+            three = range(3 * k, 3 * k + 3)
+            for i in three:
                 t, c = order[i]
-                dps_tiles[i] = bank([P, CH], F32, BANKS[i % 8])
+                dps_tiles[i] = bank([P, CH], F32, ("tp", "mm")[k % 2])
                 nc.tensor.matmul(
                     dps_tiles[i][:], lhsT=xsT[:, t * P:(t + 1) * P], rhs=wpT[:, c * CH:(c + 1) * CH],
                     start=True, stop=False,
                 )
-            for i in four:
+            for i in three:
                 t, c = order[i]
                 for q4 in range(JT):
                     nc.tensor.matmul(
@@ -384,12 +395,48 @@ def tile_multilstm_pa_kernel(
                 out=gt[:, c * CH:(c + 1) * CH], in0=gt[:, c * CH:(c + 1) * CH],
                 scalar=a_r[:, t:t + 1], in1=dps_tiles[i][:], op0=ALU.mult, op1=ALU.add,
             )
-            if c == 3:
-                nc.scalar.activation(out=gt[:, 0:2 * H], in_=gt[:, 0:2 * H], func=ACT.Sigmoid)
-            if c == 5:
-                nc.scalar.activation(out=gt[:, 2 * H:3 * H], in_=gt[:, 2 * H:3 * H], func=ACT.Tanh)
-            if c == 7:
-                nc.scalar.activation(out=gt[:, 3 * H:4 * H], in_=gt[:, 3 * H:4 * H], func=ACT.Sigmoid)
+
+        def squash(t, lo, hi, func):
+            nc.scalar.activation(out=g_sb[t][:, lo:hi], in_=g_sb[t][:, lo:hi], func=func)
+
+        def norm_o(t):
+            nc.vector.tensor_scalar(
+                out=r_sb[t][:, 3 * H:4 * H], in0=r_sb[t][:, 3 * H:4 * H], scalar1=negmu[:, t:t + 1],
+                scalar2=a_r[:, t:t + 1], op0=ALU.add, op1=ALU.mult,
+            )
+
+        def forward(p):
+            for j in (2 * p, 2 * p + 1):
+                fwd_tiles[j] = bank([P, NT, P], F32, ("gm", "misc")[j % 2])
+                for t in range(NT):
+                    nc.tensor.transpose(
+                        fwd_tiles[j][:, t, :], r_sb[t][:, 3 * H + j * P:3 * H + (j + 1) * P], ident_f[:]
+                    )
+
+        def z_exit(j):
+            nc.scalar.activation(
+                out=z_t[j // JT][:, j % JT, :], in_=fwd_tiles[j][:].rearrange("p t b -> p (t b)"), func=ACT.Identity,
+                scale=bcols[:, 2 * NJ + j:2 * NJ + j + 1], bias=bsum_col[:, 3 * OJ + j:3 * OJ + j + 1],
+            )
+
+        def o_group(t):
+            for c in (6, 7):
+                o_tiles[(t, c)] = bank([P, CH], F32, (("gm", "misc"), ("tp", "tp"), ("mm", "mm"), ("gm", "misc"))[t][c % 2])
+                nc.tensor.matmul(
+                    o_tiles[(t, c)][:], lhsT=xsT[:, t * P:(t + 1) * P], rhs=wpT[:, c * CH:(c + 1) * CH],
+                    start=True, stop=False,
+                )
+            for c in (6, 7):
+                for q4 in range(JT):
+                    nc.tensor.matmul(
+                        o_tiles[(t, c)][:, q4 * P:(q4 + 1) * P], lhsT=z_t[c - 6][:, q4, t * P:(t + 1) * P],
+                        rhs=ident_f[:], is_transpose=True, start=False, stop=(q4 == JT - 1),
+                    )
+
+        def sig_o(t, c):
+            nc.scalar.activation(
+                out=g_sb[t][:, c * CH:(c + 1) * CH], in_=o_tiles[(t, c)][:], func=ACT.Sigmoid
+            )
 
         def s_i(t):
             return g_sb[t][:, 0:H]
@@ -415,10 +462,12 @@ def tile_multilstm_pa_kernel(
                 accum_out=csum[:, t:t + 1],
             )
 
-        def stats_c(t):
+        def mean_c(t):
             nc.vector.tensor_scalar(
                 out=negmuc[:, t:t + 1], in0=csum[:, t:t + 1], scalar1=-1.0 / H, scalar2=None, op0=ALU.mult
             )
+
+        def var_c(t):
             junkc = main.tile([P, H], BF16, name="junkc", tag="junkc", bufs=1)
             nc.scalar.activation(
                 out=junkc[:], in_=t_g(t), func=ACT.Square, bias=negmuc[:, t:t + 1], scale=1.0,
@@ -441,6 +490,8 @@ def tile_multilstm_pa_kernel(
                 out=s_f(t), in0=s_i(t), scalar=a_c[:, t:t + 1], in1=lncb_bc[:], op0=ALU.mult, op1=ALU.add
             )
             nc.sync.dma_start(out=out_1[t * P:(t + 1) * P, :], in_=s_f(t))
+
+        def tanh_c(t):
             nc.scalar.activation(out=s_i(t), in_=s_f(t), func=ACT.Tanh)
 
         def new_h(t, lo, hi):
@@ -449,36 +500,66 @@ def tile_multilstm_pa_kernel(
             )
             nc.sync.dma_start(out=out_0[t * P:(t + 1) * P, lo:hi], in_=t_g(t)[:, lo:hi])
 
-        first = [(gain_r, 0, 0, 4), (fold_w, 6 * CH, G), (gain_r, 1, 0, 2)]
-        steps = [(gain_r, 1, 2, 1), (gain_r, 1, 3, 1)] + [(gain_r, t, part, 1) for t in (2, 3) for part in range(4)]
+        define("LV", [], leave_run, NJ // 2 - 1)
+        define("F3", [], fold_w, 6 * CH, G)
+        cover = {}
+        for t, part, parts in [(0, 0, 3)] + [(t, part, 1) for t in (1, 2, 3) for part in range(3)]:
+            define(("G", t, part), ["LV", ("VAR", t - 2)] if t >= 2 else [], gain_r, t, part, parts)
+            for q in range(part, part + parts):
+                cover[(t, q)] = ("G", t, part)
         for t in range(NT):
-            if t > 0:
-                steps.append((gain_c, t - 1))
-            steps.extend([(keep, t), (write, t), (state, t)])
-            if t > 0:
-                steps.append((new_c, t - 1))
-        steps.extend([
-            (gain_c, 3), (new_h, 0, 0, H), (new_h, 1, 0, H), (new_c, 3), (new_h, 2, 0, H),
-            (new_h, 3, 0, H // 2), (new_h, 3, H // 2, H),
-        ])
+            define(("VAR", t), ["LV"] if t >= 2 else [], var_r, t)
+            define(("NO", t), [("VAR", t)], norm_o, t)
+            define(("SIF", t), [("g", 6 * t + c) for c in range(4)], squash, t, 0, 2 * H, ACT.Sigmoid)
+            define(("TG", t), [("g", 6 * t + 4), ("g", 6 * t + 5)], squash, t, 2 * H, 3 * H, ACT.Tanh)
+            define(("K", t), [("SIF", t)], keep, t)
+            define(("W", t), [("SIF", t), ("TG", t)], write, t)
+            define(("S", t), [("K", t), ("W", t)], state, t)
+            define(("M", t), [("S", t)], mean_c, t)
+            define(("VC", t), [("M", t)], var_c, t)
+            define(("C1", t), [("M", t)], gain_c, t)
+            define(("C2", t), [("C1", t), ("VC", t)], new_c, t)
+            define(("TC", t), [("C2", t)], tanh_c, t)
+            define(("O", t), [("ZX", j) for j in range(OJ)] + ["F3"] + [[], [("g", 18), ("g", 19)], [("g", 21), ("g", 22)], [("SO", 0, 6), ("SO", 0, 7)]][t], o_group, t)
+            for c in (6, 7):
+                define(("SO", t, c), [("O", t)], sig_o, t, c)
+            define(("H", t), [("TC", t), ("SO", t, 6), ("SO", t, 7)], new_h, t, 0, H)
+            for half in range(2):
+                define(("H", t, half), [("TC", t), ("SO", t, 6 + half)], new_h, t, half * CH, (half + 1) * CH)
+        for i, (t, c) in enumerate(order):
+            define(("g", i), [cover[(t, c // 2)], ("T", i // 3), ("VAR", t)], gate, i)
+        for k in range(len(order) // 3):
+            define(("T", k), ["LV"] if k == 1 else [("g", i) for i in range(3 * k - 6, 3 * k - 3) if i >= 0], in_group, k)
+        for p in range(OJ // 2):
+            define(("FW", p), [("NO", t) for t in range(NT)] + [("ZX", j) for j in (2 * p - 2, 2 * p - 1) if j >= 0], forward, p)
+        for j in range(OJ):
+            define(("ZX", j), [("FW", j // 2)], z_exit, j)
 
-        var_r(0)
-        leave_run(NJ // 2 - 1)
-        input_side(0)
-        input_side(1)
-        var_r(1)
-        var_r(2)
-        for step in first:
-            step[0](*step[1:])
-        last = None
-        for n, step in enumerate(steps):
-            if n < len(order):
-                gate(n)
-                if n % 4 == 3 and n // 4 + 2 < len(order) // 4:
-                    input_side(n // 4 + 2)
-                if n == 5:
-                    var_r(3)
-            if last is not None and last[0] is state:
-                stats_c(last[1])
-            step[0](*step[1:])
-            last = step
+        vector_q = [("G", 0, 0), "F3", ("G", 1, 0)]
+        steps = [[("G", 1, 1), ("G", 1, 2), ("G", 2, 0)], [("G", 2, 1), ("G", 2, 2), ("G", 3, 0)],
+                 [("G", 3, 1), ("G", 3, 2), ("NO", 0), ("NO", 1)], [("NO", 2), ("NO", 3), ("K", 0), ("W", 0)],
+                 [("S", 0), ("K", 1), ("M", 0), ("W", 1)], [("C1", 0), ("S", 1), ("C2", 0), ("M", 1)],
+                 [("C1", 1), ("K", 2), ("W", 2)], [("S", 2), ("C2", 1), ("M", 2), ("C1", 2)]]
+        for r in range(8):
+            vector_q.extend([("g", i) for i in range(3 * r, 3 * r + 3)])
+            vector_q.extend(steps[r])
+        vector_q.extend([("K", 3), ("W", 3), ("C2", 2), ("S", 3), ("H", 0), ("M", 3), ("C1", 3), ("H", 1), ("C2", 3), ("H", 2), ("H", 3, 0), ("H", 3, 1)])
+        scalar_q = [("VAR", 0), "LV", ("VAR", 1), ("VAR", 2), ("VAR", 3), ("SIF", 0), ("TG", 0), ("SIF", 1), ("TG", 1)]
+        scalar_q.extend([("ZX", 0), ("ZX", 1), ("VC", 0), ("ZX", 2), ("ZX", 3), ("SIF", 2), ("TG", 2), ("VC", 1), ("TC", 0), ("ZX", 4), ("ZX", 5)])
+        scalar_q.extend([("ZX", 6), ("ZX", 7), ("SIF", 3), ("TC", 1), ("TG", 3), ("VC", 2), ("SO", 0, 6), ("SO", 0, 7), ("TC", 2), ("SO", 1, 6), ("SO", 1, 7)])
+        scalar_q.extend([("VC", 3), ("SO", 2, 6), ("SO", 2, 7), ("SO", 3, 6), ("TC", 3), ("SO", 3, 7)])
+        tensor_q = [("T", k) for k in range(6)] + [("FW", 0), ("T", 6), ("FW", 1), ("T", 7), ("FW", 2), ("FW", 3)]
+        tensor_q.extend([("O", t) for t in range(NT)])
+
+        done = set()
+        queues = [tensor_q, scalar_q, vector_q]
+        heads = [0, 0, 0]
+        while sum(heads) < sum(len(q) for q in queues):
+            before = sum(heads)
+            for e, q in enumerate(queues):
+                while heads[e] < len(q) and all(d in done for d in ops[q[heads[e]]][0]):
+                    deps, fn, args = ops[q[heads[e]]]
+                    fn(*args)
+                    done.add(q[heads[e]])
+                    heads[e] += 1
+            assert sum(heads) > before, "the orders wait for each other at %s" % str([q[h] for q, h in zip(queues, heads) if h < len(q)])

@@ -350,7 +350,7 @@ def tile_multilstm_pa_kernel(
             main.tile([P, JT, B], F32, name="z_t%d" % half, tag="grouped", bufs=2, align_bytes=64) for half in range(2)
         ]
 
-        def in_group(k):
+        def in_group(k, p):
             three = range(3 * k, 3 * k + 3)
             for i in three:
                 t, c = order[i]
@@ -359,6 +359,8 @@ def tile_multilstm_pa_kernel(
                     dps_tiles[i][:], lhsT=xsT[:, t * P:(t + 1) * P], rhs=wpT[:, c * CH:(c + 1) * CH],
                     start=True, stop=False,
                 )
+            if p is not None:
+                forward(p)
             for i in three:
                 t, c = order[i]
                 for q4 in range(JT):
@@ -421,7 +423,7 @@ def tile_multilstm_pa_kernel(
 
         def o_group(t):
             for c in (6, 7):
-                o_tiles[(t, c)] = bank([P, CH], F32, (("gm", "misc"), ("tp", "tp"), ("mm", "mm"), ("gm", "misc"))[t][c % 2])
+                o_tiles[(t, c)] = bank([P, CH], F32, (("tp", "tp"), ("gm", "misc"), ("mm", "mm"), ("tp", "mm"))[t][c % 2])
                 nc.tensor.matmul(
                     o_tiles[(t, c)][:], lhsT=xsT[:, t * P:(t + 1) * P], rhs=wpT[:, c * CH:(c + 1) * CH],
                     start=True, stop=False,
@@ -485,14 +487,15 @@ def tile_multilstm_pa_kernel(
                 out=s_i(t), in0=t_g(t), scalar=negmuc[:, t:t + 1], in1=lncw_bc[:], op0=ALU.add, op1=ALU.mult
             )
 
-        def new_c(t):
+        def new_c(t, lo, hi):
             nc.vector.scalar_tensor_tensor(
-                out=s_f(t), in0=s_i(t), scalar=a_c[:, t:t + 1], in1=lncb_bc[:], op0=ALU.mult, op1=ALU.add
+                out=s_f(t)[:, lo:hi], in0=s_i(t)[:, lo:hi], scalar=a_c[:, t:t + 1], in1=lncb_bc[:, lo:hi],
+                op0=ALU.mult, op1=ALU.add,
             )
-            nc.sync.dma_start(out=out_1[t * P:(t + 1) * P, :], in_=s_f(t))
+            nc.sync.dma_start(out=out_1[t * P:(t + 1) * P, lo:hi], in_=s_f(t)[:, lo:hi])
 
-        def tanh_c(t):
-            nc.scalar.activation(out=s_i(t), in_=s_f(t), func=ACT.Tanh)
+        def tanh_c(t, lo, hi):
+            nc.scalar.activation(out=s_i(t)[:, lo:hi], in_=s_f(t)[:, lo:hi], func=ACT.Tanh)
 
         def new_h(t, lo, hi):
             nc.vector.tensor_tensor(
@@ -518,22 +521,29 @@ def tile_multilstm_pa_kernel(
             define(("M", t), [("S", t)], mean_c, t)
             define(("VC", t), [("M", t)], var_c, t)
             define(("C1", t), [("M", t)], gain_c, t)
-            define(("C2", t), [("C1", t), ("VC", t)], new_c, t)
-            define(("TC", t), [("C2", t)], tanh_c, t)
-            define(("O", t), [("ZX", j) for j in range(OJ)] + ["F3"] + [[], [("g", 18), ("g", 19)], [("g", 21), ("g", 22)], [("SO", 0, 6), ("SO", 0, 7)]][t], o_group, t)
+            define(("C2", t), [("C1", t), ("VC", t)], new_c, t, 0, H)
+            define(("TC", t), [("C2", t)], tanh_c, t, 0, H)
+            define(("O", t), [("ZX", j) for j in range(OJ)] + ["F3"] + [[("g", 18), ("g", 19)], [], [("g", 21), ("g", 22)], [("g", 20), ("g", 23)]][t], o_group, t)
             for c in (6, 7):
                 define(("SO", t, c), [("O", t)], sig_o, t, c)
             define(("H", t), [("TC", t), ("SO", t, 6), ("SO", t, 7)], new_h, t, 0, H)
             for half in range(2):
-                define(("H", t, half), [("TC", t), ("SO", t, 6 + half)], new_h, t, half * CH, (half + 1) * CH)
+                define(("C2", t, half), [("C1", t), ("VC", t)], new_c, t, half * CH, (half + 1) * CH)
+                define(("TC", t, half), [("C2", t, half)], tanh_c, t, half * CH, (half + 1) * CH)
+                define(("H", t, half), [("TC", t, half), ("SO", t, 6 + half)], new_h, t, half * CH, (half + 1) * CH)
         for i, (t, c) in enumerate(order):
             define(("g", i), [cover[(t, c // 2)], ("T", i // 3), ("VAR", t)], gate, i)
         for k in range(len(order) // 3):
-            define(("T", k), ["LV"] if k == 1 else [("g", i) for i in range(3 * k - 6, 3 * k - 3) if i >= 0], in_group, k)
-        for p in range(OJ // 2):
-            define(("FW", p), [("NO", t) for t in range(NT)] + [("ZX", j) for j in (2 * p - 2, 2 * p - 1) if j >= 0], forward, p)
+            p = k - 5 if k >= 5 else None
+            define(
+                ("T", k),
+                (["LV"] if k == 1 else [("g", i) for i in range(3 * k - 6, 3 * k - 3) if i >= 0])
+                + ([("NO", t) for t in range(NT)] + [("ZX", j) for j in (2 * p - 2, 2 * p - 1) if j >= 0] if k >= 5 else []),
+                in_group, k, p,
+            )
+        define(("FW", 3), [("ZX", 4), ("ZX", 5)], forward, 3)
         for j in range(OJ):
-            define(("ZX", j), [("FW", j // 2)], z_exit, j)
+            define(("ZX", j), [("T", 5 + j // 2) if j < 6 else ("FW", 3)], z_exit, j)
 
         vector_q = [("G", 0, 0), "F3", ("G", 1, 0)]
         steps = [[("G", 1, 1), ("G", 1, 2), ("G", 2, 0)], [("G", 2, 1), ("G", 2, 2), ("G", 3, 0)],
@@ -543,12 +553,12 @@ def tile_multilstm_pa_kernel(
         for r in range(8):
             vector_q.extend([("g", i) for i in range(3 * r, 3 * r + 3)])
             vector_q.extend(steps[r])
-        vector_q.extend([("K", 3), ("W", 3), ("C2", 2), ("S", 3), ("H", 0), ("M", 3), ("C1", 3), ("H", 1), ("C2", 3), ("H", 2), ("H", 3, 0), ("H", 3, 1)])
+        vector_q.extend([("K", 3), ("H", 0), ("W", 3), ("S", 3), ("C2", 2), ("M", 3), ("H", 1), ("C1", 3), ("H", 2), ("C2", 3, 0), ("C2", 3, 1), ("H", 3, 0), ("H", 3, 1)])
         scalar_q = [("VAR", 0), "LV", ("VAR", 1), ("VAR", 2), ("VAR", 3), ("SIF", 0), ("TG", 0), ("SIF", 1), ("TG", 1)]
-        scalar_q.extend([("ZX", 0), ("ZX", 1), ("VC", 0), ("ZX", 2), ("ZX", 3), ("SIF", 2), ("TG", 2), ("VC", 1), ("TC", 0), ("ZX", 4), ("ZX", 5)])
-        scalar_q.extend([("ZX", 6), ("ZX", 7), ("SIF", 3), ("TC", 1), ("TG", 3), ("VC", 2), ("SO", 0, 6), ("SO", 0, 7), ("TC", 2), ("SO", 1, 6), ("SO", 1, 7)])
-        scalar_q.extend([("VC", 3), ("SO", 2, 6), ("SO", 2, 7), ("SO", 3, 6), ("TC", 3), ("SO", 3, 7)])
-        tensor_q = [("T", k) for k in range(6)] + [("FW", 0), ("T", 6), ("FW", 1), ("T", 7), ("FW", 2), ("FW", 3)]
+        scalar_q.extend([("ZX", 0), ("ZX", 1), ("VC", 0), ("ZX", 2), ("ZX", 3), ("SIF", 2), ("TG", 2), ("ZX", 4), ("ZX", 5), ("VC", 1), ("ZX", 6), ("ZX", 7)])
+        scalar_q.extend([("TC", 0), ("SO", 0, 6), ("SO", 0, 7), ("SIF", 3), ("SO", 1, 6), ("SO", 1, 7), ("TC", 1), ("TG", 3), ("VC", 2)])
+        scalar_q.extend([("SO", 2, 6), ("SO", 2, 7), ("SO", 3, 6), ("SO", 3, 7), ("TC", 2), ("VC", 3), ("TC", 3, 0), ("TC", 3, 1)])
+        tensor_q = [("T", k) for k in range(8)] + [("FW", 3)]
         tensor_q.extend([("O", t) for t in range(NT)])
 
         done = set()

@@ -103,8 +103,8 @@ def tile_multilstm_pa_kernel(
             out=scale_bc[:], in_=w_hh1_scale.rearrange("o k -> (o k)").partition_broadcast(P)
         )
         load_w(0, JT)
-        load_w(1, 1)
         nc.sync.dma_start(out=h0raw[:], in_=h0.rearrange("(t p) k -> p t k", p=P))
+        load_w(1, 1)
         nc.vector.memset(neg_half[:], -0.5)
         nc.vector.memset(w_nat[:, :, V:V + 2], 1.0)
         make_identity(nc, ident_f[:])
@@ -324,7 +324,7 @@ def tile_multilstm_pa_kernel(
                 leave((n - LAG) // 2, 2 * ((n - LAG) % 2))
             if n >= LAG:
                 leave((n - LAG) // 2, 2 * ((n - LAG) % 2) + 1)
-            if n == 2:
+            if n == 1:
                 for t in range(NT):
                     turn(("h", t), h0raw[:, t, :].bitcast(F32))
                     copy_out(("h", t), grouped_h, t * P)
@@ -506,7 +506,7 @@ def tile_multilstm_pa_kernel(
         define("LV", [], leave_run, NJ // 2 - 1)
         define("F3", [], fold_w, 6 * CH, G)
         cover = {}
-        for t, part, parts in [(0, 0, 3)] + [(t, part, 1) for t in (1, 2, 3) for part in range(3)]:
+        for t, part, parts in [(t, 0, 3) for t in range(NT)]:
             define(("G", t, part), ["LV", ("VAR", t - 2)] if t >= 2 else [], gain_r, t, part, parts)
             for q in range(part, part + parts):
                 cover[(t, q)] = ("G", t, part)
@@ -545,18 +545,18 @@ def tile_multilstm_pa_kernel(
         for j in range(OJ):
             define(("ZX", j), [("T", 5 + j // 2) if j < 6 else ("FW", 3)], z_exit, j)
 
-        vector_q = [("G", 0, 0), "F3", ("G", 1, 0)]
-        steps = [[("G", 1, 1), ("G", 1, 2), ("G", 2, 0)], [("G", 2, 1), ("G", 2, 2), ("G", 3, 0)],
-                 [("G", 3, 1), ("G", 3, 2), ("NO", 0), ("NO", 1)], [("NO", 2), ("NO", 3), ("K", 0), ("W", 0)],
+        vector_q = ["F3", ("G", 0, 0), ("G", 1, 0)]
+        steps = [[("G", 2, 0)], [("G", 3, 0)],
+                 [("NO", 0), ("NO", 1), ("NO", 2)], [("NO", 3), ("K", 0), ("W", 0)],
                  [("S", 0), ("K", 1), ("M", 0), ("W", 1)], [("C1", 0), ("S", 1), ("C2", 0), ("M", 1)],
-                 [("C1", 1), ("K", 2), ("W", 2)], [("S", 2), ("C2", 1), ("M", 2), ("C1", 2)]]
+                 [("C1", 1), ("K", 2), ("W", 2)], [("S", 2), ("C2", 1), ("M", 2)]]
         for r in range(8):
             vector_q.extend([("g", i) for i in range(3 * r, 3 * r + 3)])
             vector_q.extend(steps[r])
-        vector_q.extend([("K", 3), ("H", 0), ("W", 3), ("S", 3), ("C2", 2), ("M", 3), ("H", 1), ("C1", 3), ("H", 2), ("C2", 3, 0), ("C2", 3, 1), ("H", 3, 0), ("H", 3, 1)])
+        vector_q.extend([("K", 3), ("C1", 2), ("W", 3), ("C2", 2), ("S", 3), ("H", 0), ("M", 3), ("H", 1), ("C1", 3), ("H", 2), ("C2", 3, 0), ("C2", 3, 1), ("H", 3, 0), ("H", 3, 1)])
         scalar_q = [("VAR", 0), "LV", ("VAR", 1), ("VAR", 2), ("VAR", 3), ("SIF", 0), ("TG", 0), ("SIF", 1), ("TG", 1)]
         scalar_q.extend([("ZX", 0), ("ZX", 1), ("VC", 0), ("ZX", 2), ("ZX", 3), ("SIF", 2), ("TG", 2), ("ZX", 4), ("ZX", 5), ("VC", 1), ("ZX", 6), ("ZX", 7)])
-        scalar_q.extend([("TC", 0), ("SO", 0, 6), ("SO", 0, 7), ("SIF", 3), ("SO", 1, 6), ("SO", 1, 7), ("TC", 1), ("TG", 3), ("VC", 2)])
+        scalar_q.extend([("TC", 0), ("SO", 0, 6), ("SO", 0, 7), ("SIF", 3), ("TG", 3), ("VC", 2), ("TC", 1), ("SO", 1, 6), ("SO", 1, 7)])
         scalar_q.extend([("SO", 2, 6), ("SO", 2, 7), ("SO", 3, 6), ("SO", 3, 7), ("TC", 2), ("VC", 3), ("TC", 3, 0), ("TC", 3, 1)])
         tensor_q = [("T", k) for k in range(8)] + [("FW", 3)]
         tensor_q.extend([("O", t) for t in range(NT)])

@@ -81,6 +81,7 @@ def tile_multilstm_pa_kernel(
         bsum_col = main.tile([P, NJ], F32, name="bsum_col")
         neg_half = main.tile([P, NT], F32, name="neg_half")
         warm = main.tile([P, 1], F32, name="warm")
+        idle_sb = main.tile([P, 2 * P], F32, name="idle_sb")
         ident_f = main.tile([P, P], F32, name="ident_f")
         ident_b = main.tile([P, P], BF16, name="ident_b")
         h0raw = main.tile([P, NT, H], BF16, name="h0raw", tag="share_a", bufs=1)
@@ -103,8 +104,9 @@ def tile_multilstm_pa_kernel(
             out=scale_bc[:], in_=w_hh1_scale.rearrange("o k -> (o k)").partition_broadcast(P)
         )
         load_w(0, JT)
-        nc.sync.dma_start(out=h0raw[:], in_=h0.rearrange("(t p) k -> p t k", p=P))
         load_w(1, 1)
+        nc.sync.dma_start(out=h0raw[:], in_=h0.rearrange("(t p) k -> p t k", p=P))
+        nc.vector.memset(idle_sb[:], 0.0)
         nc.vector.memset(neg_half[:], -0.5)
         nc.vector.memset(w_nat[:, :, V:V + 2], 1.0)
         make_identity(nc, ident_f[:])
@@ -211,6 +213,13 @@ def tile_multilstm_pa_kernel(
                 op0=ALU.add, op1=ALU.mult,
             )
 
+        def keep_warm():
+            idle_ps = bank([P, 2 * P], F32, "mm")
+            nc.tensor.matmul(idle_ps[:], lhsT=idle_sb[:, 0:P], rhs=idle_sb[:], start=True, stop=True)
+
+        for idle in range(4):
+            keep_warm()
+
         for n in range(NJ // 2):
             if n in (2, 4, 6, 8):
                 load_w(n // 2 + 3, 1)
@@ -246,19 +255,23 @@ def tile_multilstm_pa_kernel(
                     scales=hscl[:].rearrange("p g c -> p (g c)"),
                     in_=grouped_h[:].rearrange("p g c -> p (g c)"),
                 )
-            if n == 12:
-                nc.vector.tensor_tensor(out=ysc[:], in0=side["yp"][:], in1=x_nat[:], op=ALU.mult)
             if n == 13:
                 nc.vector.tensor_scalar(out=vae[:], in0=va[:], scalar1=EPS, scalar2=None, op0=ALU.add)
                 nc.gpsimd.tensor_tensor(out=a_a[:], in0=vae[:], in1=neg_half[:], op=ALU.pow)
             if n >= 2 and n % 2 == 0:
                 quant_w((n - 2) // 2)
+            if n == 12:
+                nc.vector.tensor_tensor(out=ysc[:], in0=side["yp"][:], in1=x_nat[:], op=ALU.mult)
 
             split = n % 2 == 1 and n > LAG
             turn_w(2 * n)
+            if n < LAG:
+                keep_warm()
             if n >= LAG and split:
                 mult((n - LAG) // 2, 2 * ((n - LAG) % 2))
             turn_w(2 * n + 1)
+            if n < LAG:
+                keep_warm()
             if n == 3:
                 xps = bank([P, NT, P], BF16, "misc")
                 for t in range(NT):
@@ -328,6 +341,8 @@ def tile_multilstm_pa_kernel(
                 for t in range(NT):
                     turn(("h", t), h0raw[:, t, :].bitcast(F32))
                     copy_out(("h", t), grouped_h, t * P)
+                    if t % 2 == 1:
+                        keep_warm()
 
         fold_w(0, 3 * CH)
         quant_w(NCH - 1)
@@ -530,7 +545,7 @@ def tile_multilstm_pa_kernel(
             for half in range(2):
                 define(("C2", t, half), [("C1", t), ("VC", t)], new_c, t, half * CH, (half + 1) * CH)
                 define(("TC", t, half), [("C2", t, half)], tanh_c, t, half * CH, (half + 1) * CH)
-                define(("H", t, half), [("TC", t, half), ("SO", t, 6 + half)], new_h, t, half * CH, (half + 1) * CH)
+                define(("H", t, half), [("TC", t, half) if t == NT - 1 else ("TC", t), ("SO", t, 6 + half)], new_h, t, half * CH, (half + 1) * CH)
         for i, (t, c) in enumerate(order):
             define(("g", i), [cover[(t, c // 2)], ("T", i // 3), ("VAR", t)], gate, i)
         for k in range(len(order) // 3):
@@ -553,7 +568,7 @@ def tile_multilstm_pa_kernel(
         for r in range(8):
             vector_q.extend([("g", i) for i in range(3 * r, 3 * r + 3)])
             vector_q.extend(steps[r])
-        vector_q.extend([("K", 3), ("C1", 2), ("W", 3), ("C2", 2), ("S", 3), ("H", 0), ("M", 3), ("H", 1), ("C1", 3), ("H", 2), ("C2", 3, 0), ("C2", 3, 1), ("H", 3, 0), ("H", 3, 1)])
+        vector_q.extend([("H", 0), ("C1", 2), ("K", 3), ("W", 3), ("C2", 2), ("S", 3), ("H", 1, 0), ("M", 3), ("H", 1, 1), ("C1", 3), ("H", 2), ("C2", 3, 0), ("C2", 3, 1), ("H", 3, 0), ("H", 3, 1)])
         scalar_q = [("VAR", 0), "LV", ("VAR", 1), ("VAR", 2), ("VAR", 3), ("SIF", 0), ("TG", 0), ("SIF", 1), ("TG", 1)]
         scalar_q.extend([("ZX", 0), ("ZX", 1), ("VC", 0), ("ZX", 2), ("ZX", 3), ("SIF", 2), ("TG", 2), ("ZX", 4), ("ZX", 5), ("VC", 1), ("ZX", 6), ("ZX", 7)])
         scalar_q.extend([("TC", 0), ("SO", 0, 6), ("SO", 0, 7), ("SIF", 3), ("TG", 3), ("VC", 2), ("TC", 1), ("SO", 1, 6), ("SO", 1, 7)])

@@ -130,9 +130,11 @@ def tile_multilstm_pa_kernel(
 
         def widen(k):
             wbf = main.tile([P, H], BF16, name="wbf", tag="wbf", bufs=6)
-            nc.vector.tensor_tensor(
-                out=wbf[:], in0=wb_tiles[k // JT][:, k % JT, :].bitcast(FP8), in1=scale_bc[:], op=ALU.mult
-            )
+            for lo in (0, H // 2):
+                nc.vector.tensor_tensor(
+                    out=wbf[:, lo:lo + H // 2], in0=wb_tiles[k // JT][:, k % JT, lo:lo + H // 2].bitcast(FP8),
+                    in1=scale_bc[:, lo:lo + H // 2], op=ALU.mult,
+                )
             wbf_tiles[k] = wbf
 
         def turn(key, words):
@@ -164,11 +166,10 @@ def tile_multilstm_pa_kernel(
         def quant_w(c):
             wcod = main.tile([P, 2, CH], U32, name="wcod", tag="wcod", bufs=2, align_bytes=64)
             wscl = main.tile([P, 2, CH], U8, name="wscl", tag="wscl", bufs=2, align_bytes=64)
-            nc.vector.quantize_mx(
-                out=wcod[:].rearrange("p g c -> p (g c)").bitcast(FP8X4),
-                scales=wscl[:].rearrange("p g c -> p (g c)"),
-                in_=grouped_tiles[c][:].rearrange("p g c -> p (g c)"),
-            )
+            for g2 in range(2):
+                nc.vector.quantize_mx(
+                    out=wcod[:, g2, :].bitcast(FP8X4), scales=wscl[:, g2, :], in_=grouped_tiles[c][:, g2, :]
+                )
             cod_tiles[c] = (wcod, wscl)
 
         def mult(c, t):
@@ -542,6 +543,10 @@ def tile_multilstm_pa_kernel(
             for c in (6, 7):
                 define(("SO", t, c), [("O", t)], sig_o, t, c)
             define(("H", t), [("TC", t), ("SO", t, 6), ("SO", t, 7)], new_h, t, 0, H)
+            for q in range(4):
+                define(("C2q", t, q), [("C1", t), ("VC", t)], new_c, t, q * 256, (q + 1) * 256)
+                define(("TCq", t, q), [("C2q", t, q)], tanh_c, t, q * 256, (q + 1) * 256)
+                define(("Hq", t, q), [("TCq", t, q), ("SO", t, 6 + q // 2)], new_h, t, q * 256, (q + 1) * 256)
             for half in range(2):
                 define(("C2", t, half), [("C1", t), ("VC", t)], new_c, t, half * CH, (half + 1) * CH)
                 define(("TC", t, half), [("C2", t, half)], tanh_c, t, half * CH, (half + 1) * CH)
@@ -568,11 +573,11 @@ def tile_multilstm_pa_kernel(
         for r in range(8):
             vector_q.extend([("g", i) for i in range(3 * r, 3 * r + 3)])
             vector_q.extend(steps[r])
-        vector_q.extend([("H", 0), ("C1", 2), ("K", 3), ("W", 3), ("C2", 2), ("S", 3), ("H", 1, 0), ("M", 3), ("H", 1, 1), ("C1", 3), ("H", 2), ("C2", 3, 0), ("C2", 3, 1), ("H", 3, 0), ("H", 3, 1)])
+        vector_q.extend([("H", 0), ("C1", 2), ("K", 3), ("W", 3), ("C2", 2), ("S", 3), ("H", 1, 0), ("M", 3), ("H", 1, 1), ("C1", 3), ("H", 2), ("C2q", 3, 0), ("C2q", 3, 1), ("C2q", 3, 2), ("C2q", 3, 3), ("Hq", 3, 0), ("Hq", 3, 1), ("Hq", 3, 2), ("Hq", 3, 3)])
         scalar_q = [("VAR", 0), "LV", ("VAR", 1), ("VAR", 2), ("VAR", 3), ("SIF", 0), ("TG", 0), ("SIF", 1), ("TG", 1)]
         scalar_q.extend([("ZX", 0), ("ZX", 1), ("VC", 0), ("ZX", 2), ("ZX", 3), ("SIF", 2), ("TG", 2), ("ZX", 4), ("ZX", 5), ("VC", 1), ("ZX", 6), ("ZX", 7)])
         scalar_q.extend([("TC", 0), ("SO", 0, 6), ("SO", 0, 7), ("SIF", 3), ("TG", 3), ("VC", 2), ("TC", 1), ("SO", 1, 6), ("SO", 1, 7)])
-        scalar_q.extend([("SO", 2, 6), ("SO", 2, 7), ("SO", 3, 6), ("SO", 3, 7), ("TC", 2), ("VC", 3), ("TC", 3, 0), ("TC", 3, 1)])
+        scalar_q.extend([("SO", 2, 6), ("SO", 2, 7), ("SO", 3, 6), ("SO", 3, 7), ("TC", 2), ("VC", 3), ("TCq", 3, 0), ("TCq", 3, 1), ("TCq", 3, 2), ("TCq", 3, 3)])
         tensor_q = [("T", k) for k in range(8)] + [("FW", 3)]
         tensor_q.extend([("O", t) for t in range(NT)])
 

from contextlib import ExitStack

import concourse.mybir as mybir
from concourse.masks import make_identity

B, V, H = 512, 128, 1024
G = 4 * H
EPS = 1e-5
FLOPS = 2 * B * G * (H + V)

F32 = mybir.dt.float32
BF16 = mybir.dt.bfloat16
U8 = mybir.dt.uint8
U32 = mybir.dt.uint32
FP8 = mybir.dt.float8_e4m3fn
FP8X4 = mybir.dt.float8_e4m3fn_x4
ALU = mybir.AluOpType
ACT = mybir.ActivationFunctionType
AX = mybir.AxisListType

P = 128
NT = B // P
CH = 512
NCH = G // CH
JT = CH // P
NJ = G // P
LAG = 3
VPAD = 144
OJ = H // P
BUFS = {"tp": 3, "mm": 3, "gm": 1, "misc": 1}


def tile_multilstm_pa_kernel(
    tc, x, h0, c0, w_ih1, w_hh1_bytes, w_hh1_scale,
    lni_w1, lni_b1, lnh_w1, lnh_b1, lnc_w1, lnc_b1, out_0, out_1,
):
    nc = tc.nc
    with ExitStack() as ctx:
        main = ctx.enter_context(tc.tile_pool(name="main", bufs=1))
        psum = ctx.enter_context(tc.psum_pool(name="psum", bufs=1))
        ctx.enter_context(tc.manual_schedule())

        def bank(shape, dtype, tag):
            return psum.tile(shape, dtype, name="ps_" + tag, tag=tag, bufs=BUFS[tag])

        scale_bc = main.tile([P, H], F32, name="scale_bc")
        wh_bc = main.tile([P, G], BF16, name="wh_bc")
        wi_bc = main.tile([P, G], BF16, name="wi_bc")
        lncw_bc = main.tile([P, H], BF16, name="lncw_bc")
        lncb_bc = main.tile([P, H], BF16, name="lncb_bc")
        wpT = main.tile([P, G], F32, name="wpT")
        xT = main.tile([P, B], F32, name="xT")
        xs = main.tile([P, NT, V], F32, name="xs")
        xsT = main.tile([P, B], F32, name="xsT")
        x_nat = main.tile([P, NT, V], BF16, name="x_nat")
        ysc = main.tile([P, NT, V], F32, name="ysc")
        craw = main.tile([P, V + 2], F32, name="craw")
        c_sb = main.tile([P, V], F32, name="c_sb")
        colsrc = main.tile([P, P], BF16, name="colsrc")
        hcod = main.tile([P, 2, B], U32, name="hcod", align_bytes=64)
        hscl = main.tile([P, 2, B], U8, name="hscl", align_bytes=64)
        ring = [main.tile([P, G], F32, name="ring%d" % t) for t in range(NT + 2)]
        r_sb = ring[0:NT]
        g_sb = ring[NT:NT + 2] + ring[0:NT - 2]
        rsum = main.tile([P, NT, NCH], F32, name="rsum")
        rtot = main.tile([P, NT, NCH], F32, name="rtot")
        negmu = main.tile([P, NT], F32, name="negmu")
        rvs = main.tile([P, NT], F32, name="rvs")
        rve = main.tile([P, NT], F32, name="rve")
        a_r = main.tile([P, NT], F32, name="a_r")
        va = main.tile([P, NT], F32, name="va")
        vae = main.tile([P, NT], F32, name="vae")
        a_a = main.tile([P, NT], F32, name="a_a")
        csum = main.tile([P, NT], F32, name="csum")
        negmuc = main.tile([P, NT], F32, name="negmuc")
        cvs = main.tile([P, NT], F32, name="cvs")
        cve = main.tile([P, NT], F32, name="cve")
        a_c = main.tile([P, NT], F32, name="a_c")
        negwbar = main.tile([P, 1], F32, name="negwbar")
        bcols = main.tile([P, 2 * NJ + OJ], F32, name="bcols")
        bsum_col = main.tile([P, NJ], F32, name="bsum_col")
        neg_half = main.tile([P, NT], F32, name="neg_half")
        warm = main.tile([P, 1], F32, name="warm")
        idle_sb = main.tile([P, 2 * P], F32, name="idle_sb")
        ident_f = main.tile([P, P], F32, name="ident_f")
        ident_b = main.tile([P, P], BF16, name="ident_b")
        h0raw = main.tile([P, NT, H], BF16, name="h0raw", tag="share_a", bufs=1)
        grouped_h = main.tile([P, 2, 4 * B], BF16, name="grouped_h", tag="share_b", bufs=1, align_bytes=64)
        w_nat = main.tile([P, NJ, VPAD], BF16, name="w_nat", tag="share_c", bufs=1)

        wb_tiles = {}

        def load_w(c, pieces):
            wb = main.tile([P, JT, H], U8, name="wb", tag="wb", bufs=4)
            src = w_hh1_bytes[c * CH:(c + 1) * CH, :].rearrange("(j p) k -> p j k", p=P)
            step_j = JT // pieces
            for i in range(pieces):
                nc.sync.dma_start(
                    out=wb[:, i * step_j:(i + 1) * step_j, :], in_=src[:, i * step_j:(i + 1) * step_j, :]
                )
            wb_tiles[c] = wb

        nc.sync.dma_start(
            out=scale_bc[:], in_=w_hh1_scale.rearrange("o k -> (o k)").partition_broadcast(P)
        )
        load_w(0, JT)
        load_w(1, 1)
        nc.sync.dma_start(out=h0raw[:], in_=h0.rearrange("(t p) k -> p t k", p=P))
        nc.vector.memset(idle_sb[:], 0.0)
        nc.vector.memset(neg_half[:], -0.5)
        nc.vector.memset(w_nat[:, :, V:V + 2], 1.0)
        make_identity(nc, ident_f[:])
        make_identity(nc, ident_b[:])
        nc.gpsimd.memset(colsrc[:], 0.0)
        nc.scalar.activation(out=warm[:], in_=neg_half[:, 0:1], func=ACT.Sigmoid)
        nc.sync.dma_start(out=x_nat[:], in_=x.rearrange("(t p) v -> p t v", p=P))
        nc.sync.dma_start(out=colsrc[0:NJ, :], in_=lni_b1.rearrange("(j p) -> j p", p=P))
        nc.sync.dma_start(out=colsrc[NJ:2 * NJ, :], in_=lnh_b1.rearrange("(j p) -> j p", p=P))
        nc.sync.dma_start(out=colsrc[2 * NJ:2 * NJ + OJ, :], in_=lnh_w1[3 * H:4 * H].rearrange("(j p) -> j p", p=P))
        load_w(2, 1)
        nc.sync.dma_start(out=w_nat[:, :, 0:V], in_=w_ih1.rearrange("(j p) v -> p j v", p=P))
        load_w(3, 1)
        nc.sync.dma_start(out=wi_bc[:], in_=lni_w1.partition_broadcast(P))

        wbf_tiles = {}
        tp_tiles = {}
        grouped_tiles = {}
        cod_tiles = {}
        mm_tiles = {}

        def widen(k):
            wbf = main.tile([P, H], BF16, name="wbf", tag="wbf", bufs=6)
            for lo in (0, H // 2):
                nc.vector.tensor_tensor(
                    out=wbf[:, lo:lo + H // 2], in0=wb_tiles[k // JT][:, k % JT, lo:lo + H // 2].bitcast(FP8),
                    in1=scale_bc[:, lo:lo + H // 2], op=ALU.mult,
                )
            wbf_tiles[k] = wbf

        def turn(key, words):
            tp = bank([P, 4, P], F32, "tp")
            for g2 in range(2):
                for u in range(2):
                    nc.tensor.transpose(
                        tp[:, 2 * g2 + u, :], words[:, 256 * g2 + u:256 * (g2 + 1):2], ident_f[:]
                    )
            tp_tiles[key] = tp

        def copy_out(key, grouped, col0):
            gw = grouped[:].bitcast(F32).rearrange("p g (c u) -> p g c u", u=2)
            nc.scalar.copy(
                out=gw[:, :, col0:col0 + P, :],
                in_=tp_tiles[key][:].rearrange("p (g u) r -> p g r u", u=2),
            )

        def turn_w(k):
            turn(k, wbf_tiles[k][:].bitcast(F32))

        def copy_w(k):
            if k % JT == 0:
                grouped_tiles[k // JT] = main.tile(
                    [P, 2, 4 * CH], BF16, name="grouped", tag="grouped", bufs=2, align_bytes=64
                )
            copy_out(k, grouped_tiles[k // JT], (k % JT) * P)

        def quant_w(c):
            wcod = main.tile([P, 2, CH], U32, name="wcod", tag="wcod", bufs=2, align_bytes=64)
            wscl = main.tile([P, 2, CH], U8, name="wscl", tag="wscl", bufs=2, align_bytes=64)
            for g2 in range(2):
                nc.vector.quantize_mx(
                    out=wcod[:, g2, :].bitcast(FP8X4), scales=wscl[:, g2, :], in_=grouped_tiles[c][:, g2, :]
                )
            cod_tiles[c] = (wcod, wscl)

        def mult(c, t):
            wcod, wscl = cod_tiles[c]
            mm = bank([P, CH], F32, "mm")
            for g2 in range(2):
                nc.tensor.matmul_mx(
                    out=mm[:],
                    lhsT=hcod[:, g2, t * P:(t + 1) * P].bitcast(FP8X4),
                    lhsT_scale=hscl[:, g2, t * P:(t + 1) * P],
                    rhs=wcod[:, g2, :].bitcast(FP8X4),
                    rhs_scale=wscl[:, g2, :],
                    start=(g2 == 0),
                    stop=(g2 == 1),
                )
            mm_tiles[(c, t)] = mm

        def leave(c, t):
            nc.scalar.activation(
                out=r_sb[t][:, c * CH:(c + 1) * CH], in_=mm_tiles[(c, t)][:], func=ACT.Copy,
                accum_out=rsum[:, t, c:c + 1],
            )
            if c == NCH - 1:
                nc.scalar.activation(
                    out=rtot[:, t, :], in_=rsum[:, t, :], func=ACT.Copy, scale=-1.0 / G,
                    accum_out=negmu[:, t:t + 1],
                )

        def mult_run(m):
            for t in (2 * (m % 2), 2 * (m % 2) + 1):
                mult(m // 2, t)

        def leave_run(m):
            for t in (2 * (m % 2), 2 * (m % 2) + 1):
                leave(m // 2, t)

        side = {}

        def fold_w(lo, hi):
            nc.vector.scalar_tensor_tensor(
                out=wpT[:, lo:hi], in0=side["w_t"][:, lo:hi], scalar=negwbar[:, 0:1], in1=wi_bc[:, lo:hi],
                op0=ALU.add, op1=ALU.mult,
            )

        def keep_warm():
            idle_ps = bank([P, 2 * P], F32, "mm")
            nc.tensor.matmul(idle_ps[:], lhsT=idle_sb[:, 0:P], rhs=idle_sb[:], start=True, stop=True)

        for idle in range(4):
            keep_warm()

        for n in range(NJ // 2):
            if n in (2, 4, 6, 8):
                load_w(n // 2 + 3, 1)
            if n == 2:
                nc.sync.dma_start(out=wh_bc[:], in_=lnh_w1.partition_broadcast(P))
            if n == 4:
                nc.sync.dma_start(out=lncw_bc[:], in_=lnc_w1.partition_broadcast(P))
                nc.sync.dma_start(out=lncb_bc[:], in_=lnc_b1.partition_broadcast(P))
            if n == 12:
                side["c0"] = main.tile([P, NT, H], BF16, name="c0_sb", tag="share_c", bufs=1)
                nc.sync.dma_start(out=side["c0"][:], in_=c0.rearrange("(t p) k -> p t k", p=P))

            widen(2 * n)
            if n == 5:
                nc.vector.tensor_tensor(
                    out=bsum_col[:], in0=bcols[:, 0:NJ], in1=bcols[:, NJ:2 * NJ], op=ALU.add
                )
            if n == 9:
                nc.vector.tensor_scalar(
                    out=negwbar[:], in0=craw[:, V:V + 1], scalar1=-1.0, scalar2=None, op0=ALU.mult
                )
            if n == 11:
                nc.vector.scalar_tensor_tensor(
                    out=c_sb[:], in0=side["nb"][:], scalar=craw[:, V:V + 1], in1=craw[:, 0:V],
                    op0=ALU.mult, op1=ALU.add,
                )
            if n == 13:
                nc.vector.tensor_reduce(out=va[:], in_=ysc[:], axis=AX.X, op=ALU.add)
            widen(2 * n + 1)
            if n == 3:
                nc.vector.quantize_mx(
                    out=hcod[:].rearrange("p g c -> p (g c)").bitcast(FP8X4),
                    scales=hscl[:].rearrange("p g c -> p (g c)"),
                    in_=grouped_h[:].rearrange("p g c -> p (g c)"),
                )
            if n == 13:
                nc.vector.tensor_scalar(out=vae[:], in0=va[:], scalar1=EPS, scalar2=None, op0=ALU.add)
                nc.gpsimd.tensor_tensor(out=a_a[:], in0=vae[:], in1=neg_half[:], op=ALU.pow)
            if n >= 2 and n % 2 == 0:
                quant_w((n - 2) // 2)
            if n == 12:
                nc.vector.tensor_tensor(out=ysc[:], in0=side["yp"][:], in1=x_nat[:], op=ALU.mult)

            split = n % 2 == 1 and n > LAG
            turn_w(2 * n)
            if n < LAG:
                keep_warm()
            if n >= LAG and split:
                mult((n - LAG) // 2, 2 * ((n - LAG) % 2))
            turn_w(2 * n + 1)
            if n < LAG:
                keep_warm()
            if n == 3:
                xps = bank([P, NT, P], BF16, "misc")
                for t in range(NT):
                    nc.tensor.transpose(xps[:, t, :], x_nat[:, t, :], ident_b[:])
                cps = bank([P, P], BF16, "gm")
                nc.tensor.transpose(cps[:], colsrc[:], ident_b[:])
            if 4 <= n < 12:
                wps = bank([P, JT, P], BF16, "misc")
                for q in range(JT):
                    nc.tensor.transpose(wps[:, q, :], w_nat[:, JT * (n - 4) + q, 0:V], ident_b[:])
            if n == 15:
                xsps = bank([P, NT, P], F32, "misc")
                for t in range(NT):
                    nc.tensor.transpose(xsps[:, t, :], xs[:, t, :], ident_f[:])
            if n == 9:
                side["nb"] = bank([P, V], F32, "gm")
                nc.tensor.matmul(
                    side["nb"][:], lhsT=negwbar[:, 0:1].to_broadcast([P, P]), rhs=ident_f[:],
                    start=True, stop=True,
                )
            if n == 11:
                side["yp"] = bank([P, NT, V], F32, "gm")
                for t in range(NT):
                    nc.tensor.matmul(
                        side["yp"][:, t, :], lhsT=xT[:, t * P:(t + 1) * P], rhs=c_sb[:], start=True, stop=True
                    )
            if n >= LAG and not split:
                mult((n - LAG) // 2, 2 * ((n - LAG) % 2))
            if n >= LAG:
                mult((n - LAG) // 2, 2 * ((n - LAG) % 2) + 1)
            if 4 <= n < 8:
                if n == 4:
                    side["gm"] = bank([P, V + 2], F32, "gm")
                for j in range(8 * (n - 4), 8 * (n - 3)):
                    nc.tensor.matmul(
                        side["gm"][:], lhsT=w_nat[:, j, 0:V], rhs=w_nat[:, j, 0:V + 2],
                        start=(j == 0), stop=(j == NJ - 1),
                    )

            if n == 8:
                nc.scalar.activation(out=craw[:], in_=side["gm"][:], func=ACT.Copy, scale=1.0 / G)
            copy_w(2 * n)
            if n >= LAG and split:
                leave((n - LAG) // 2, 2 * ((n - LAG) % 2))
            copy_w(2 * n + 1)
            if n == 3:
                nc.scalar.copy(out=xT[:], in_=xps[:].rearrange("p t b -> p (t b)"))
                nc.scalar.copy(out=bcols[:], in_=cps[:, 0:2 * NJ + OJ])
            if 4 <= n < 12:
                if n == 4:
                    side["w_t"] = main.tile([P, G], BF16, name="w_t", tag="share_b", bufs=1, align_bytes=64)
                nc.scalar.copy(
                    out=side["w_t"][:, (n - 4) * CH:(n - 3) * CH], in_=wps[:].rearrange("p q g -> p (q g)")
                )
            if n == 14:
                for t in range(NT):
                    nc.scalar.activation(
                        out=xs[:, t, :], in_=x_nat[:, t, :], func=ACT.Copy, scale=a_a[:, t:t + 1]
                    )
            if n == 15:
                nc.scalar.copy(out=xsT[:], in_=xsps[:].rearrange("p t b -> p (t b)"))
            if n >= LAG and not split:
                leave((n - LAG) // 2, 2 * ((n - LAG) % 2))
            if n >= LAG:
                leave((n - LAG) // 2, 2 * ((n - LAG) % 2) + 1)
            if n == 1:
                for t in range(NT):
                    turn(("h", t), h0raw[:, t, :].bitcast(F32))
                    copy_out(("h", t), grouped_h, t * P)
                    if t % 2 == 1:
                        keep_warm()

        fold_w(0, 3 * CH)
        quant_w(NCH - 1)
        fold_w(3 * CH, 6 * CH)
        for m in range(NJ // 2 - LAG, NJ // 2 - 1):
            mult_run(m)
            leave_run(m)
        mult_run(NJ // 2 - 1)

        ops = {}

        def define(name, deps, fn, *args):
            ops[name] = (deps, fn, args)

        order = [(t, c) for t in range(NT) for c in range(6)]
        dps_tiles = {}
        fwd_tiles = {}
        o_tiles = {}
        z_t = [
            main.tile([P, JT, B], F32, name="z_t%d" % half, tag="grouped", bufs=2, align_bytes=64) for half in range(2)
        ]

        def in_group(k, p):
            three = range(3 * k, 3 * k + 3)
            for i in three:
                t, c = order[i]
                dps_tiles[i] = bank([P, CH], F32, ("tp", "mm")[k % 2])
                nc.tensor.matmul(
                    dps_tiles[i][:], lhsT=xsT[:, t * P:(t + 1) * P], rhs=wpT[:, c * CH:(c + 1) * CH],
                    start=True, stop=False,
                )
            if p is not None:
                forward(p)
            for i in three:
                t, c = order[i]
                for q4 in range(JT):
                    nc.tensor.matmul(
                        dps_tiles[i][:, q4 * P:(q4 + 1) * P],
                        lhsT=bsum_col[:, JT * c + q4:JT * c + q4 + 1].to_broadcast([P, P]), rhs=ident_f[:],
                        is_transpose=True, start=False, stop=(q4 == JT - 1),
                    )

        def var_r(t):
            junk = main.tile([P, G], BF16, name="junk", tag="share_a", bufs=1)
            nc.scalar.activation(
                out=junk[:], in_=r_sb[t][:], func=ACT.Square, bias=negmu[:, t:t + 1], scale=1.0,
                accum_out=rvs[:, t:t + 1],
            )
            nc.scalar.activation(
                out=rve[:, t:t + 1], in_=rvs[:, t:t + 1], func=ACT.Copy, scale=1.0 / G, bias=EPS
            )
            nc.gpsimd.tensor_tensor(
                out=a_r[:, t:t + 1], in0=rve[:, t:t + 1], in1=neg_half[:, 0:1], op=ALU.pow
            )

        def gain_r(t, part, parts):
            cols = slice(part * H, (part + parts) * H)
            nc.vector.scalar_tensor_tensor(
                out=g_sb[t][:, cols], in0=r_sb[t][:, cols], scalar=negmu[:, t:t + 1], in1=wh_bc[:, cols],
                op0=ALU.add, op1=ALU.mult,
            )

        def gate(i):
            t, c = order[i]
            gt = g_sb[t]
            nc.vector.scalar_tensor_tensor(
                out=gt[:, c * CH:(c + 1) * CH], in0=gt[:, c * CH:(c + 1) * CH],
                scalar=a_r[:, t:t + 1], in1=dps_tiles[i][:], op0=ALU.mult, op1=ALU.add,
            )

        def squash(t, lo, hi, func):
            nc.scalar.activation(out=g_sb[t][:, lo:hi], in_=g_sb[t][:, lo:hi], func=func)

        def norm_o(t):
            nc.vector.tensor_scalar(
                out=r_sb[t][:, 3 * H:4 * H], in0=r_sb[t][:, 3 * H:4 * H], scalar1=negmu[:, t:t + 1],
                scalar2=a_r[:, t:t + 1], op0=ALU.add, op1=ALU.mult,
            )

        def forward(p):
            for j in (2 * p, 2 * p + 1):
                fwd_tiles[j] = bank([P, NT, P], F32, ("gm", "misc")[j % 2])
                for t in range(NT):
                    nc.tensor.transpose(
                        fwd_tiles[j][:, t, :], r_sb[t][:, 3 * H + j * P:3 * H + (j + 1) * P], ident_f[:]
                    )

        def z_exit(j):
            nc.scalar.activation(
                out=z_t[j // JT][:, j % JT, :], in_=fwd_tiles[j][:].rearrange("p t b -> p (t b)"), func=ACT.Identity,
                scale=bcols[:, 2 * NJ + j:2 * NJ + j + 1], bias=bsum_col[:, 3 * OJ + j:3 * OJ + j + 1],
            )

        def o_group(t):
            for c in (6, 7):
                o_tiles[(t, c)] = bank([P, CH], F32, (("tp", "tp"), ("gm", "misc"), ("mm", "mm"), ("tp", "mm"))[t][c % 2])
                nc.tensor.matmul(
                    o_tiles[(t, c)][:], lhsT=xsT[:, t * P:(t + 1) * P], rhs=wpT[:, c * CH:(c + 1) * CH],
                    start=True, stop=False,
                )
            for c in (6, 7):
                for q4 in range(JT):
                    nc.tensor.matmul(
                        o_tiles[(t, c)][:, q4 * P:(q4 + 1) * P], lhsT=z_t[c - 6][:, q4, t * P:(t + 1) * P],
                        rhs=ident_f[:], is_transpose=True, start=False, stop=(q4 == JT - 1),
                    )

        def sig_o(t, c):
            nc.scalar.activation(
                out=g_sb[t][:, c * CH:(c + 1) * CH], in_=o_tiles[(t, c)][:], func=ACT.Sigmoid
            )

        def s_i(t):
            return g_sb[t][:, 0:H]

        def s_f(t):
            return g_sb[t][:, H:2 * H]

        def t_g(t):
            return g_sb[t][:, 2 * H:3 * H]

        def s_o(t):
            return g_sb[t][:, 3 * H:4 * H]

        def keep(t):
            nc.vector.tensor_tensor(out=s_f(t), in0=s_f(t), in1=side["c0"][:, t, :], op=ALU.mult)

        def write(t):
            nc.vector.tensor_tensor(out=s_i(t), in0=s_i(t), in1=t_g(t), op=ALU.mult)

        def state(t):
            nc.vector.scalar_tensor_tensor(
                out=t_g(t), in0=s_i(t), scalar=1.0, in1=s_f(t), op0=ALU.mult, op1=ALU.add,
                accum_out=csum[:, t:t + 1],
            )

        def mean_c(t):
            nc.vector.tensor_scalar(
                out=negmuc[:, t:t + 1], in0=csum[:, t:t + 1], scalar1=-1.0 / H, scalar2=None, op0=ALU.mult
            )

        def var_c(t):
            junkc = main.tile([P, H], BF16, name="junkc", tag="junkc", bufs=1)
            nc.scalar.activation(
                out=junkc[:], in_=t_g(t), func=ACT.Square, bias=negmuc[:, t:t + 1], scale=1.0,
                accum_out=cvs[:, t:t + 1],
            )
            nc.scalar.activation(
                out=cve[:, t:t + 1], in_=cvs[:, t:t + 1], func=ACT.Copy, scale=1.0 / H, bias=EPS
            )
            nc.gpsimd.tensor_tensor(
                out=a_c[:, t:t + 1], in0=cve[:, t:t + 1], in1=neg_half[:, 0:1], op=ALU.pow
            )

        def gain_c(t):
            nc.vector.scalar_tensor_tensor(
                out=s_i(t), in0=t_g(t), scalar=negmuc[:, t:t + 1], in1=lncw_bc[:], op0=ALU.add, op1=ALU.mult
            )

        def new_c(t, lo, hi):
            nc.vector.scalar_tensor_tensor(
                out=s_f(t)[:, lo:hi], in0=s_i(t)[:, lo:hi], scalar=a_c[:, t:t + 1], in1=lncb_bc[:, lo:hi],
                op0=ALU.mult, op1=ALU.add,
            )
            nc.sync.dma_start(out=out_1[t * P:(t + 1) * P, lo:hi], in_=s_f(t)[:, lo:hi])

        def tanh_c(t, lo, hi):
            nc.scalar.activation(out=s_i(t)[:, lo:hi], in_=s_f(t)[:, lo:hi], func=ACT.Tanh)

        def new_h(t, lo, hi):
            nc.vector.tensor_tensor(
                out=t_g(t)[:, lo:hi], in0=s_o(t)[:, lo:hi], in1=s_i(t)[:, lo:hi], op=ALU.mult
            )
            nc.sync.dma_start(out=out_0[t * P:(t + 1) * P, lo:hi], in_=t_g(t)[:, lo:hi])

        define("LV", [], leave_run, NJ // 2 - 1)
        define("F3", [], fold_w, 6 * CH, G)
        cover = {}
        for t, part, parts in [(t, 0, 3) for t in range(NT)]:
            define(("G", t, part), ["LV", ("VAR", t - 2)] if t >= 2 else [], gain_r, t, part, parts)
            for q in range(part, part + parts):
                cover[(t, q)] = ("G", t, part)
        for t in range(NT):
            define(("VAR", t), ["LV"] if t >= 2 else [], var_r, t)
            define(("NO", t), [("VAR", t)], norm_o, t)
            define(("SIF", t), [("g", 6 * t + c) for c in range(4)], squash, t, 0, 2 * H, ACT.Sigmoid)
            define(("TG", t), [("g", 6 * t + 4), ("g", 6 * t + 5)], squash, t, 2 * H, 3 * H, ACT.Tanh)
            define(("K", t), [("SIF", t)], keep, t)
            define(("W", t), [("SIF", t), ("TG", t)], write, t)
            define(("S", t), [("K", t), ("W", t)], state, t)
            define(("M", t), [("S", t)], mean_c, t)
            define(("VC", t), [("M", t)], var_c, t)
            define(("C1", t), [("M", t)], gain_c, t)
            define(("C2", t), [("C1", t), ("VC", t)], new_c, t, 0, H)
            define(("TC", t), [("C2", t)], tanh_c, t, 0, H)
            define(("O", t), [("ZX", j) for j in range(OJ)] + ["F3"] + [[("g", 18), ("g", 19)], [], [("g", 21), ("g", 22)], [("g", 20), ("g", 23)]][t], o_group, t)
            for c in (6, 7):
                define(("SO", t, c), [("O", t)], sig_o, t, c)
            define(("H", t), [("TC", t), ("SO", t, 6), ("SO", t, 7)], new_h, t, 0, H)
            for q in range(4):
                define(("C2q", t, q), [("C1", t), ("VC", t)], new_c, t, q * 256, (q + 1) * 256)
                define(("TCq", t, q), [("C2q", t, q)], tanh_c, t, q * 256, (q + 1) * 256)
                define(("Hq", t, q), [("TCq", t, q), ("SO", t, 6 + q // 2)], new_h, t, q * 256, (q + 1) * 256)
            for half in range(2):
                define(("C2", t, half), [("C1", t), ("VC", t)], new_c, t, half * CH, (half + 1) * CH)
                define(("TC", t, half), [("C2", t, half)], tanh_c, t, half * CH, (half + 1) * CH)
                define(("H", t, half), [("TC", t, half) if t == NT - 1 else ("TC", t), ("SO", t, 6 + half)], new_h, t, half * CH, (half + 1) * CH)
        for i, (t, c) in enumerate(order):
            define(("g", i), [cover[(t, c // 2)], ("T", i // 3), ("VAR", t)], gate, i)
        for k in range(len(order) // 3):
            p = k - 5 if k >= 5 else None
            define(
                ("T", k),
                (["LV"] if k == 1 else [("g", i) for i in range(3 * k - 6, 3 * k - 3) if i >= 0])
                + ([("NO", t) for t in range(NT)] + [("ZX", j) for j in (2 * p - 2, 2 * p - 1) if j >= 0] if k >= 5 else []),
                in_group, k, p,
            )
        define(("FW", 3), [("ZX", 4), ("ZX", 5)], forward, 3)
        for j in range(OJ):
            define(("ZX", j), [("T", 5 + j // 2) if j < 6 else ("FW", 3)], z_exit, j)

        vector_q = ["F3", ("G", 0, 0), ("G", 1, 0)]
        steps = [[("G", 2, 0)], [("G", 3, 0)],
                 [("NO", 0), ("NO", 1), ("NO", 2)], [("NO", 3), ("K", 0), ("W", 0)],
                 [("S", 0), ("K", 1), ("M", 0), ("W", 1)], [("C1", 0), ("S", 1), ("C2", 0), ("M", 1)],
                 [("C1", 1), ("K", 2), ("W", 2)], [("S", 2), ("C2", 1), ("M", 2)]]
        for r in range(8):
            vector_q.extend([("g", i) for i in range(3 * r, 3 * r + 3)])
            vector_q.extend(steps[r])
        vector_q.extend([("H", 0), ("C1", 2), ("K", 3), ("W", 3), ("C2", 2), ("S", 3), ("H", 1, 0), ("M", 3), ("H", 1, 1), ("C1", 3), ("H", 2), ("C2q", 3, 0), ("C2q", 3, 1), ("C2q", 3, 2), ("C2q", 3, 3), ("Hq", 3, 0), ("Hq", 3, 1), ("Hq", 3, 2), ("Hq", 3, 3)])
        scalar_q = [("VAR", 0), "LV", ("VAR", 1), ("VAR", 2), ("VAR", 3), ("SIF", 0), ("TG", 0), ("SIF", 1), ("TG", 1)]
        scalar_q.extend([("ZX", 0), ("ZX", 1), ("VC", 0), ("ZX", 2), ("ZX", 3), ("SIF", 2), ("TG", 2), ("ZX", 4), ("ZX", 5), ("VC", 1), ("ZX", 6), ("ZX", 7)])
        scalar_q.extend([("TC", 0), ("SO", 0, 6), ("SO", 0, 7), ("SIF", 3), ("TG", 3), ("VC", 2), ("TC", 1), ("SO", 1, 6), ("SO", 1, 7)])
        scalar_q.extend([("SO", 2, 6), ("SO", 2, 7), ("SO", 3, 6), ("SO", 3, 7), ("TC", 2), ("VC", 3), ("TCq", 3, 0), ("TCq", 3, 1), ("TCq", 3, 2), ("TCq", 3, 3)])
        tensor_q = [("T", k) for k in range(8)] + [("FW", 3)]
        tensor_q.extend([("O", t) for t in range(NT)])

        done = set()
        queues = [tensor_q, scalar_q, vector_q]
        heads = [0, 0, 0]
        while sum(heads) < sum(len(q) for q in queues):
            before = sum(heads)
            for e, q in enumerate(queues):
                while heads[e] < len(q) and all(d in done for d in ops[q[heads[e]]][0]):
                    deps, fn, args = ops[q[heads[e]]]
                    fn(*args)
                    done.add(q[heads[e]])
                    heads[e] += 1
            assert sum(heads) > before, "the orders wait for each other at %s" % str([q[h] for q, h in zip(queues, heads) if h < len(q)])
